import numpy as np
import ml_dtypes


def mxq(x, axis, fmt="e4m3"):
    dtype, down = {"e4m3": (ml_dtypes.float8_e4m3fn, 7), "e5m2": (ml_dtypes.float8_e5m2, 14)}[fmt]
    v = np.moveaxis(np.asarray(x, np.float32).astype(ml_dtypes.bfloat16).astype(np.float64), axis, -1)
    blocks = v.reshape(v.shape[:-1] + (-1, 32))
    amax = np.abs(blocks).max(-1, keepdims=True)
    byte = np.maximum(np.where(amax > 0, np.frexp(amax)[1] - 1 + 127, 0) - down, 1)
    scale = np.exp2(byte - 127.0)
    codes = (blocks / scale).astype(np.float32).astype(dtype).astype(np.float64)
    return np.moveaxis((codes * scale).reshape(v.shape), -1, axis)


WIDE = False


def mx_kscale(k):
    if not WIDE:
        return np.ones(k)
    levels = np.array([10, -10, 5, -5, 0])
    if k % 512:
        return np.exp2(np.random.permutation(np.resize(levels, k // 32))).repeat(32)
    a = np.empty((k // 512, 16))
    for p in range(k // 512):
        a[p, :8] = np.random.permutation(np.resize(levels, 8))
        for g in range(8):
            far = levels[np.abs(levels - a[p, g]) >= 10]
            a[p, g + 8] = far[np.random.randint(len(far))]
    return np.exp2(a.ravel()).repeat(32)


BF16 = ml_dtypes.bfloat16


def bf(x):
    return np.asarray(x, np.float32).astype(BF16)


def f64(x):
    return np.asarray(x).astype(np.float64)


B, T, C, H, D = 4, 1024, 1024, 2, 128
HD = H * D
EPS = 2.0 ** -23
ROPE_BASE = 2.0 ** 10
BOUND = np.sqrt(3.0) * 0.5 / np.sqrt(C)


def rope_tables():
    freq = np.concatenate([(1.0 / ROPE_BASE) ** np.linspace(0.0, 1.0, D // 4), np.zeros(D // 4)])
    theta = f64(np.arange(T))[:, None] * freq[None, :]
    return np.cos(theta), np.sin(theta)


def apply_rope(u, cos, sin):
    u1, u2 = u[..., : D // 2], u[..., D // 2 :]
    c, s = cos[None, :, None, :], sin[None, :, None, :]
    return np.concatenate([u1 * c + u2 * s, u2 * c - u1 * s], axis=-1)


def rms_norm(u):
    return u / np.sqrt(np.mean(np.square(u), axis=-1, keepdims=True) + EPS)


def setup_inputs():
    s = mx_kscale(C)
    return {"x": bf(np.random.standard_normal((B, T, C)) * s),
            "ve": bf(np.random.standard_normal((B, T, HD))),
            "qkv_w": bf(np.random.uniform(-BOUND, BOUND, (3, HD, C)) / s),
            "lambdas": bf(0.5 + 0.1 * np.random.standard_normal(2))}


def reference(x, ve, qkv_w, lambdas):
    w = f64(qkv_w).reshape(3 * HD, C)
    qkv = (mxq(f64(x), 2, "e4m3") @ mxq(w, 1, "e4m3").T).reshape(B, T, 3, H, D)
    q, k, v = qkv[:, :, 0], qkv[:, :, 1], qkv[:, :, 2]
    cos, sin = rope_tables()
    q = apply_rope(rms_norm(q), cos, sin)
    k = apply_rope(rms_norm(k), cos, sin)
    lam = f64(lambdas)
    v = lam[0] * v + lam[1] * f64(ve).reshape(B, T, H, D)
    return q, k, v

@@ -1,0 +1,353 @@
+import math
+from contextlib import ExitStack
+
+import concourse.bass as bass
+import concourse.mybir as mybir
+import concourse.tile as tile
+from concourse.masks import make_identity
+
+F32 = mybir.dt.float32
+BF16 = mybir.dt.bfloat16
+I32 = mybir.dt.int32
+U32 = mybir.dt.uint32
+U8 = mybir.dt.uint8
+FP8X4 = mybir.dt.float8_e4m3fn_x4
+ALU = mybir.AluOpType
+ACT = mybir.ActivationFunctionType
+
+B, T, C, H, D = 4, 1024, 1024, 2, 128
+HD = H * D
+P = 128
+J = T // P
+NPAIR = B * J // 2
+EPS = 2.0 ** -23
+FLOPS = 2 * B * T * C * 3 * HD
+MANUAL = True
+VE_ON_SCALAR = (1, 3)
+
+
+def tile_causalselfattention_pa_t_kernel(tc, x, ve, qkv_w, lambdas, out_0, out_1, out_2):
+    nc = tc.nc
+    x_v = x.rearrange("b (p j) c -> b p j c", j=J)
+    ve_v = ve.rearrange("b (p j) f -> b p j f", j=J)
+    w_v = qkv_w.rearrange("s (r p) c -> p (s r) c", p=P)
+    o_v = [o.rearrange("b (p j) h d -> b p j (h d)", j=J) for o in (out_0, out_1, out_2)]
+
+    with ExitStack() as ctx:
+        const = ctx.enter_context(tc.tile_pool(name="const", bufs=1))
+        xin = ctx.enter_context(tc.tile_pool(name="xin", bufs=B))
+        outp = ctx.enter_context(tc.tile_pool(name="outp", bufs=3))
+        work = ctx.enter_context(tc.tile_pool(name="work", bufs=3))
+        small = ctx.enter_context(tc.tile_pool(name="small", bufs=4))
+        ps_xt = ctx.enter_context(tc.psum_pool(name="ps_xt", bufs=2))
+        ps_qk = ctx.enter_context(tc.psum_pool(name="ps_qk", bufs=4))
+        ps_v = ctx.enter_context(tc.psum_pool(name="ps_v", bufs=2))
+        if MANUAL:
+            ctx.enter_context(tc.manual_schedule())
+
+        ident = const.tile([P, P], F32, name="ident")
+        make_identity(nc, ident[:])
+        tpos_i = const.tile([P, J], I32, name="tpos_i")
+        nc.gpsimd.iota(tpos_i[:], pattern=[[1, J]], base=0, channel_multiplier=J)
+
+        lam_bf = const.tile([P, 2], BF16, name="lam_bf")
+        nc.scalar.dma_start(out=lam_bf[:], in_=lambdas.partition_broadcast(P))
+        w_sb = const.tile([P, 6, C], BF16, name="w_sb")
+        x_sb = [xin.tile([P, J, C], BF16, name="x_sb") for b in range(B)]
+        ve_sb = [xin.tile([P, J, HD], BF16, name="ve_sb") for b in range(B)]
+        nc.sync.dma_start(out=w_sb[:, 0:2, :], in_=w_v[:, 0:2, :])
+        nc.sync.dma_start(out=w_sb[:, 2:4, :], in_=w_v[:, 2:4, :])
+        nc.sync.dma_start(out=x_sb[0][:, 0:2, :], in_=x_v[0][:, 0:2, :])
+        nc.sync.dma_start(out=w_sb[:, 4:6, :], in_=w_v[:, 4:6, :])
+        nc.sync.dma_start(out=x_sb[0][:, 2:4, :], in_=x_v[0][:, 2:4, :])
+        nc.sync.dma_start(out=ve_sb[0][:], in_=ve_v[0])
+        nc.sync.dma_start(out=x_sb[0][:, 4:8, :], in_=x_v[0][:, 4:8, :])
+        for b in range(1, B):
+            nc.sync.dma_start(out=x_sb[b][:, 0:4, :], in_=x_v[b][:, 0:4, :])
+            nc.sync.dma_start(out=ve_sb[b][:], in_=ve_v[b])
+            nc.sync.dma_start(out=x_sb[b][:, 4:8, :], in_=x_v[b][:, 4:8, :])
+
+        zero1 = const.tile([P, 1], F32, name="zero1")
+        nc.vector.memset(zero1[:], 0.0)
+        warm = const.tile([P, 1], F32, name="warm")
+        nc.scalar.activation(out=warm[:], in_=zero1[:], func=ACT.Sin)
+        ratio = (1.0 / 1024.0) ** (1.0 / 31.0)
+        turns = const.tile([P, 32], F32, name="turns")
+        for i in range(8):
+            nc.vector.tensor_scalar_add(out=turns[:, i : i + 1], in0=zero1[:], scalar1=ratio ** i / (2.0 * math.pi))
+        nc.vector.tensor_scalar_mul(out=turns[:, 8:16], in0=turns[:, 0:8], scalar1=ratio ** 8)
+        nc.vector.tensor_scalar_mul(out=turns[:, 16:32], in0=turns[:, 0:16], scalar1=ratio ** 16)
+        tpos = const.tile([P, J], F32, name="tpos")
+        nc.vector.tensor_copy(out=tpos[:], in_=tpos_i[:])
+        ang = const.tile([P, J, 32], F32, name="ang")
+        nc.vector.tensor_tensor(
+            out=ang[:],
+            in0=tpos[:].unsqueeze(2).to_broadcast([P, J, 32]),
+            in1=turns[:].unsqueeze(1).to_broadcast([P, J, 32]),
+            op=ALU.mult,
+        )
+        whole_i = const.tile([P, J, 32], I32, name="whole_i")
+        nc.vector.tensor_copy(out=whole_i[:], in_=ang[:])
+        whole = const.tile([P, J, 32], F32, name="whole")
+        nc.vector.tensor_copy(out=whole[:], in_=whole_i[:])
+        frac = const.tile([P, J * 32], F32, name="frac")
+        nc.vector.tensor_sub(
+            out=frac[:], in0=ang[:].rearrange("p j i -> p (j i)"), in1=whole[:].rearrange("p j i -> p (j i)")
+        )
+        negf = const.tile([P, J * 32], F32, name="negf")
+        nc.vector.scalar_tensor_tensor(
+            out=negf[:], in0=frac[:], scalar=0.5, in1=frac[:], op0=ALU.is_gt, op1=ALU.subtract
+        )
+        absf = const.tile([P, J * 32], F32, name="absf")
+        nc.vector.scalar_tensor_tensor(
+            out=absf[:], in0=negf[:], scalar=-1.0, in1=negf[:], op0=ALU.mult, op1=ALU.max
+        )
+        c_exp = const.tile([P, J, 4, 32], F32, name="c_exp")
+        s_exp = const.tile([P, J, 2, 2, 32], F32, name="s_exp")
+        nc.scalar.activation(
+            out=c_exp[:],
+            in_=absf[:].rearrange("p (j i) -> p j i", j=J).unsqueeze(2).to_broadcast([P, J, 4, 32]),
+            func=ACT.Sin,
+            scale=-2.0 * math.pi,
+            bias=0.5 * math.pi,
+        )
+        for z in range(2):
+            nc.scalar.activation(
+                out=s_exp[:, :, :, z, :],
+                in_=negf[:].rearrange("p (j i) -> p j i", j=J).unsqueeze(2).to_broadcast([P, J, 2, 32]),
+                func=ACT.Sin,
+                scale=(2.0 * z - 1.0) * 2.0 * math.pi,
+            )
+        lam = const.tile([P, 2], F32, name="lam")
+
+        wg = const.tile([P, 2, 3 * HD, 4], BF16, name="wg", align_bytes=64)
+        wgf = wg[:].bitcast(F32)
+        wc = const.tile([P, 2, 3 * HD], U32, name="wc", align_bytes=64)
+        ws = const.tile([P, 2, 3 * HD], U8, name="ws", align_bytes=64)
+        w_words = w_sb[:].bitcast(F32)
+
+        def w_transpose(r):
+            if r < 4:
+                wt = ps_qk.tile([P, 4, P], F32, name="wt", tag="qk")
+            else:
+                wt = ps_v.tile([P, 4, P], F32, name="wt", tag="v")
+            for q in range(4):
+                nc.tensor.transpose(wt[:, q, :], w_words[:, r, (q // 2) * 256 + q % 2 : (q // 2 + 1) * 256 : 2], ident[:])
+            return wt
+
+        def w_copy(r, wt, eng):
+            dst = wgf[:, :, r * P : (r + 1) * P, :]
+            src = wt[:].rearrange("p (g u) n -> p g n u", u=2)
+            if eng == "s":
+                nc.scalar.copy(out=dst, in_=src)
+            else:
+                nc.vector.tensor_copy(out=dst, in_=src)
+
+        def w_quant(g, n0, n1):
+            nc.vector.quantize_mx(
+                out=wc[:, g, n0:n1].bitcast(FP8X4),
+                scales=ws[:, g, n0:n1],
+                in_=wg[:, g, n0:n1, :].rearrange("p n t -> p (n t)"),
+            )
+
+        xt_t = {}
+        grp_t = {}
+        xc_t = {}
+        xs_t = {}
+        qk_t = {}
+        v_t = {}
+        ss_t = {}
+        r_t = {}
+        qk_sb = {}
+        v_sb = {}
+
+        def where(n):
+            return n // 4, 2 * (n % 4)
+
+        def transposes(n):
+            b, j0 = where(n)
+            xw = x_sb[b][:].bitcast(F32)
+            for s in range(2):
+                xt = ps_xt.tile([P, 4, P], F32, name="xt", tag="xt")
+                for q in range(4):
+                    nc.tensor.transpose(xt[:, q, :], xw[:, j0 + s, (q // 2) * 256 + q % 2 : (q // 2 + 1) * 256 : 2], ident[:])
+                xt_t[(n, s)] = xt
+
+        def x_copy(n, engs):
+            grp = work.tile([P, 2, 2, P, 4], BF16, name="grp", align_bytes=64)
+            grp_t[n] = grp
+            gf = grp[:].bitcast(F32)
+            for s in range(2):
+                src = xt_t[(n, s)][:].rearrange("p (g u) m -> p g m u", u=2)
+                if engs[s] == "s":
+                    nc.scalar.copy(out=gf[:, s, :, :, :], in_=src)
+                else:
+                    nc.vector.tensor_copy(out=gf[:, s, :, :, :], in_=src)
+
+        def x_quant(n):
+            xc = work.tile([P, 2, 2, P], U32, name="xc", align_bytes=64)
+            xs = work.tile([P, 2, 2, P], U8, name="xs", align_bytes=64)
+            xc_t[n] = xc
+            xs_t[n] = xs
+            nc.vector.quantize_mx(
+                out=xc[:].rearrange("p s g m -> p (s g m)").bitcast(FP8X4),
+                scales=xs[:].rearrange("p s g m -> p (s g m)"),
+                in_=grp_t[n][:].rearrange("p s g m t -> p (s g m t)"),
+            )
+
+        def matmuls(n):
+            xc = xc_t[n]
+            xs = xs_t[n]
+            vps = ps_v.tile([P, 2, HD], F32, name="vps", tag="v")
+            v_t[n] = vps
+            for s in range(2):
+                qkps = ps_qk.tile([P, 2 * HD], F32, name="qkps", tag="qk")
+                qk_t[(n, s)] = qkps
+                for g in range(2):
+                    nc.tensor.matmul_mx(
+                        out=qkps[:],
+                        lhsT=xc[:, s, g, :].bitcast(FP8X4),
+                        lhsT_scale=xs[:, s, g, :],
+                        rhs=wc[:, g, 0 : 2 * HD].bitcast(FP8X4),
+                        rhs_scale=ws[:, g, 0 : 2 * HD],
+                        start=(g == 0),
+                        stop=(g == 1),
+                    )
+                    nc.tensor.matmul_mx(
+                        out=vps[:, s, :],
+                        lhsT=xc[:, s, g, :].bitcast(FP8X4),
+                        lhsT_scale=xs[:, s, g, :],
+                        rhs=wc[:, g, 2 * HD : 3 * HD].bitcast(FP8X4),
+                        rhs_scale=ws[:, g, 2 * HD : 3 * HD],
+                        start=(g == 0),
+                        stop=(g == 1),
+                    )
+
+        def ve_scale(n):
+            b, j0 = where(n)
+            if j0 == 0:
+                v_sb[b] = outp.tile([P, J, HD], F32, name="v_sb")
+            dst = v_sb[b][:, j0 : j0 + 2, :]
+            src = ve_sb[b][:, j0 : j0 + 2, :]
+            if n % 4 in VE_ON_SCALAR:
+                nc.scalar.activation(out=dst, in_=src, func=ACT.Copy, scale=lam[:, 1:2])
+            else:
+                nc.vector.tensor_scalar_mul(out=dst, in0=src, scalar1=lam[:, 1:2])
+
+        def v_blend(n):
+            b, j0 = where(n)
+            dst = v_sb[b][:, j0 : j0 + 2, :].rearrange("p j f -> p (j f)")
+            nc.vector.scalar_tensor_tensor(
+                out=dst,
+                in0=v_t[n][:].rearrange("p s f -> p (s f)"),
+                scalar=lam[:, 0:1],
+                in1=dst,
+                op0=ALU.mult,
+                op1=ALU.add,
+            )
+
+        junk = const.tile([P, D], BF16, name="junk")
+
+        def sumsq(n):
+            ss = small.tile([P, 8], F32, name="ss")
+            ss_t[n] = ss
+            for s in range(2):
+                for c in range(4):
+                    nc.scalar.activation(
+                        out=junk[:],
+                        in_=qk_t[(n, s)][:, c * D : (c + 1) * D],
+                        func=ACT.Square,
+                        accum_out=ss[:, 4 * s + c : 4 * s + c + 1],
+                    )
+            sd = small.tile([P, 8], F32, name="sd")
+            nc.scalar.activation(out=sd[:], in_=ss[:], func=ACT.Sqrt, scale=1.0 / D, bias=EPS)
+            ss_t[n] = sd
+
+        def normalise(n):
+            b, j0 = where(n)
+            if j0 == 0:
+                qk_sb[b] = outp.tile([P, 2, J, HD], F32, name="qk_sb")
+            r = small.tile([P, 8], F32, name="r")
+            nc.vector.reciprocal(out=r[:], in_=ss_t[n][:])
+            for s in range(2):
+                nc.vector.tensor_tensor(
+                    out=qk_sb[b][:, :, j0 + s, :].rearrange("p a (h d) -> p a h d", h=H),
+                    in0=qk_t[(n, s)][:].rearrange("p (a h d) -> p a h d", a=2, h=H),
+                    in1=r[:, 4 * s : 4 * s + 4]
+                    .rearrange("p (a h) -> p a h", a=2)
+                    .unsqueeze(3)
+                    .to_broadcast([P, 2, H, D]),
+                    op=ALU.mult,
+                )
+
+        def rope(n):
+            b, j0 = where(n)
+            nv4 = qk_sb[b][:, :, j0 : j0 + 2, :].rearrange("p a j (h z f) -> p a (j h) z f", h=H, z=2)[:, :, :, :, 0:32]
+            nv = qk_sb[b][:, :, j0 : j0 + 2, :].rearrange("p a j (q f) -> p a (j q) f", q=4)[:, :, :, 0:32]
+            t1 = work.tile([P, 2, 8, 32], F32, name="t1")
+            t2 = work.tile([P, 2, 4, 2, 32], F32, name="t2")
+            nc.vector.tensor_tensor(
+                out=t1[:],
+                in0=nv,
+                in1=c_exp[:, j0 : j0 + 2, :, :].rearrange("p j q i -> p (j q) i").unsqueeze(1).to_broadcast([P, 2, 8, 32]),
+                op=ALU.mult,
+            )
+            for z in range(2):
+                nc.vector.tensor_tensor(
+                    out=t2[:, :, :, z, :],
+                    in0=nv4[:, :, :, 1 - z, :],
+                    in1=s_exp[:, j0 : j0 + 2, :, z, :].rearrange("p j h i -> p (j h) i").unsqueeze(1).to_broadcast([P, 2, 4, 32]),
+                    op=ALU.mult,
+                )
+            nc.vector.tensor_tensor(
+                out=nv, in0=t1[:], in1=t2[:].rearrange("p a q z i -> p a (q z) i"), op=ALU.add
+            )
+
+        def stores(n):
+            b, j0 = where(n)
+            if j0 % 4 == 2:
+                js = slice(j0 - 2, j0 + 2)
+                nc.sync.dma_start(out=o_v[2][b][:, js, :], in_=v_sb[b][:, js, :])
+                nc.sync.dma_start(out=o_v[0][b][:, js, :], in_=qk_sb[b][:, 0, js, :])
+                nc.sync.dma_start(out=o_v[1][b][:, js, :], in_=qk_sb[b][:, 1, js, :])
+
+        wts = [w_transpose(r) for r in range(4)]
+        transposes(0)
+        wts.append(w_transpose(4))
+        wts.append(w_transpose(5))
+        w_copy(0, wts[0], "s")
+        w_copy(1, wts[1], "v")
+        w_copy(2, wts[2], "s")
+        w_copy(3, wts[3], "v")
+        x_copy(0, "sv")
+        w_quant(0, 0, 2 * HD)
+        w_copy(4, wts[4], "s")
+        w_copy(5, wts[5], "v")
+        w_quant(1, 0, 2 * HD)
+        x_quant(0)
+        w_quant(0, 2 * HD, 3 * HD)
+        w_quant(1, 2 * HD, 3 * HD)
+        nc.scalar.activation(out=warm[:], in_=zero1[:], func=ACT.Sqrt, bias=1.0)
+        transposes(1)
+        x_copy(1, "ss")
+        nc.vector.tensor_copy(out=lam[:], in_=lam_bf[:])
+        ve_scale(0)
+        ve_scale(1)
+
+        for n in range(NPAIR):
+            matmuls(n)
+            if n + 2 < NPAIR:
+                transposes(n + 2)
+            if n + 1 < NPAIR:
+                x_quant(n + 1)
+            v_blend(n)
+            if n >= 1:
+                rope(n - 1)
+                stores(n - 1)
+            sumsq(n)
+            if n + 2 < NPAIR:
+                x_copy(n + 2, "ss")
+                ve_scale(n + 2)
+            normalise(n)
+        rope(NPAIR - 1)
+        stores(NPAIR - 1)

@@ -23,7 +23,7 @@ NPAIR = B * J // 2
 EPS = 2.0 ** -23
 FLOPS = 2 * B * T * C * 3 * HD
 MANUAL = True
-VE_ON_SCALAR = (1, 3)
+VE_ON_SCALAR = (0, 1, 2, 3)
 
 
 def tile_causalselfattention_pa_t_kernel(tc, x, ve, qkv_w, lambdas, out_0, out_1, out_2):
@@ -102,22 +102,20 @@ def tile_causalselfattention_pa_t_kernel(tc, x, ve, qkv_w, lambdas, out_0, out_1
         nc.vector.scalar_tensor_tensor(
             out=absf[:], in0=negf[:], scalar=-1.0, in1=negf[:], op0=ALU.mult, op1=ALU.max
         )
-        c_exp = const.tile([P, J, 4, 32], F32, name="c_exp")
-        s_exp = const.tile([P, J, 2, 2, 32], F32, name="s_exp")
+        cs = const.tile([P, J, 2, 32], F32, name="cs")
         nc.scalar.activation(
-            out=c_exp[:],
-            in_=absf[:].rearrange("p (j i) -> p j i", j=J).unsqueeze(2).to_broadcast([P, J, 4, 32]),
+            out=cs[:, :, 0, :],
+            in_=absf[:].rearrange("p (j i) -> p j i", j=J),
             func=ACT.Sin,
             scale=-2.0 * math.pi,
             bias=0.5 * math.pi,
         )
-        for z in range(2):
-            nc.scalar.activation(
-                out=s_exp[:, :, :, z, :],
-                in_=negf[:].rearrange("p (j i) -> p j i", j=J).unsqueeze(2).to_broadcast([P, J, 2, 32]),
-                func=ACT.Sin,
-                scale=(2.0 * z - 1.0) * 2.0 * math.pi,
-            )
+        nc.scalar.activation(
+            out=cs[:, :, 1, :],
+            in_=negf[:].rearrange("p (j i) -> p j i", j=J),
+            func=ACT.Sin,
+            scale=-2.0 * math.pi,
+        )
         lam = const.tile([P, 2], F32, name="lam")
 
         wg = const.tile([P, 2, 3 * HD, 4], BF16, name="wg", align_bytes=64)
@@ -156,7 +154,8 @@ def tile_causalselfattention_pa_t_kernel(tc, x, ve, qkv_w, lambdas, out_0, out_1
         xs_t = {}
         qk_t = {}
         v_t = {}
-        ss_t = {}
+        rcs_t = {}
+        t_t = {}
         r_t = {}
         qk_sb = {}
         v_sb = {}
@@ -246,61 +245,73 @@ def tile_causalselfattention_pa_t_kernel(tc, x, ve, qkv_w, lambdas, out_0, out_1
                 op1=ALU.add,
             )
 
-        junk = const.tile([P, D], BF16, name="junk")
-
         def sumsq(n):
             ss = small.tile([P, 8], F32, name="ss")
-            ss_t[n] = ss
+            junk = work.tile([P, 8, D], BF16, name="junk")
             for s in range(2):
                 for c in range(4):
                     nc.scalar.activation(
-                        out=junk[:],
+                        out=junk[:, 4 * s + c, :],
                         in_=qk_t[(n, s)][:, c * D : (c + 1) * D],
                         func=ACT.Square,
                         accum_out=ss[:, 4 * s + c : 4 * s + c + 1],
                     )
-            sd = small.tile([P, 8], F32, name="sd")
-            nc.scalar.activation(out=sd[:], in_=ss[:], func=ACT.Sqrt, scale=1.0 / D, bias=EPS)
-            ss_t[n] = sd
+            r = small.tile([P, 8], F32, name="r")
+            nc.scalar.activation(out=r[:], in_=ss[:], func=ACT.Abs_reciprocal_sqrt, scale=1.0 / D, bias=EPS)
+            r_t[n] = r
 
-        def normalise(n):
+        def scaled_tables(n):
+            b, j0 = where(n)
+            rcs = work.tile([P, 8, 2, 32], F32, name="rcs")
+            rcs_t[n] = rcs
+            nc.gpsimd.tensor_tensor(
+                out=rcs[:].rearrange("p (s q) t i -> p s q (t i)", s=2),
+                in0=cs[:, j0 : j0 + 2, :, :].rearrange("p j t i -> p j (t i)").unsqueeze(2).to_broadcast([P, 2, 4, 64]),
+                in1=r_t[n][:].rearrange("p (s q) -> p s q", s=2).unsqueeze(3).to_broadcast([P, 2, 4, 64]),
+                op=ALU.mult,
+            )
+
+        def products(n):
+            t = work.tile([P, 2, 2, 2, H, 2, 32], F32, name="t")
+            t_t[n] = t
+            for s in range(2):
+                u = qk_t[(n, s)][:].rearrange("p (a h z f) -> p a h z f", a=2, h=H, z=2)[:, :, :, :, 0:32]
+                for e in range(2):
+                    nc.vector.tensor_tensor(
+                        out=t[:, e, :, s, :, :, :],
+                        in0=u,
+                        in1=rcs_t[n][:, 4 * s : 4 * s + 4, e, :]
+                        .rearrange("p (a h) i -> p a h i", a=2)
+                        .unsqueeze(3)
+                        .to_broadcast([P, 2, H, 2, 32]),
+                        op=ALU.mult,
+                    )
+
+        def passthrough(n):
+            b, j0 = where(n)
+            for s in range(2):
+                nc.vector.tensor_tensor(
+                    out=qk_sb[b][:, :, j0 + s, :].rearrange("p a (h z f) -> p a h z f", h=H, z=2)[:, :, :, :, 32:64],
+                    in0=qk_t[(n, s)][:].rearrange("p (a h z f) -> p a h z f", a=2, h=H, z=2)[:, :, :, :, 32:64],
+                    in1=r_t[n][:, 4 * s : 4 * s + 4]
+                    .rearrange("p (a h) -> p a h", a=2)
+                    .unsqueeze(3)
+                    .unsqueeze(4)
+                    .to_broadcast([P, 2, H, 2, 32]),
+                    op=ALU.mult,
+                )
+
+        def combine(n):
             b, j0 = where(n)
             if j0 == 0:
                 qk_sb[b] = outp.tile([P, 2, J, HD], F32, name="qk_sb")
-            r = small.tile([P, 8], F32, name="r")
-            nc.vector.reciprocal(out=r[:], in_=ss_t[n][:])
-            for s in range(2):
-                nc.vector.tensor_tensor(
-                    out=qk_sb[b][:, :, j0 + s, :].rearrange("p a (h d) -> p a h d", h=H),
-                    in0=qk_t[(n, s)][:].rearrange("p (a h d) -> p a h d", a=2, h=H),
-                    in1=r[:, 4 * s : 4 * s + 4]
-                    .rearrange("p (a h) -> p a h", a=2)
-                    .unsqueeze(3)
-                    .to_broadcast([P, 2, H, D]),
-                    op=ALU.mult,
-                )
-
-        def rope(n):
-            b, j0 = where(n)
-            nv4 = qk_sb[b][:, :, j0 : j0 + 2, :].rearrange("p a j (h z f) -> p a (j h) z f", h=H, z=2)[:, :, :, :, 0:32]
-            nv = qk_sb[b][:, :, j0 : j0 + 2, :].rearrange("p a j (q f) -> p a (j q) f", q=4)[:, :, :, 0:32]
-            t1 = work.tile([P, 2, 8, 32], F32, name="t1")
-            t2 = work.tile([P, 2, 4, 2, 32], F32, name="t2")
+            y = qk_sb[b][:, :, j0 : j0 + 2, :].rearrange("p a j (h z f) -> p a (j h) z f", h=H, z=2)
+            t = t_t[n][:].rearrange("p e a s h z i -> p e a (s h) z i")
             nc.vector.tensor_tensor(
-                out=t1[:],
-                in0=nv,
-                in1=c_exp[:, j0 : j0 + 2, :, :].rearrange("p j q i -> p (j q) i").unsqueeze(1).to_broadcast([P, 2, 8, 32]),
-                op=ALU.mult,
+                out=y[:, :, :, 0, 0:32], in0=t[:, 0, :, :, 0, :], in1=t[:, 1, :, :, 1, :], op=ALU.add
             )
-            for z in range(2):
-                nc.vector.tensor_tensor(
-                    out=t2[:, :, :, z, :],
-                    in0=nv4[:, :, :, 1 - z, :],
-                    in1=s_exp[:, j0 : j0 + 2, :, z, :].rearrange("p j h i -> p (j h) i").unsqueeze(1).to_broadcast([P, 2, 4, 32]),
-                    op=ALU.mult,
-                )
             nc.vector.tensor_tensor(
-                out=nv, in0=t1[:], in1=t2[:].rearrange("p a q z i -> p a (q z) i"), op=ALU.add
+                out=y[:, :, :, 1, 0:32], in0=t[:, 0, :, :, 1, :], in1=t[:, 1, :, :, 0, :], op=ALU.subtract
             )
 
         def stores(n):
@@ -327,27 +338,32 @@ def tile_causalselfattention_pa_t_kernel(tc, x, ve, qkv_w, lambdas, out_0, out_1
         x_quant(0)
         w_quant(0, 2 * HD, 3 * HD)
         w_quant(1, 2 * HD, 3 * HD)
-        nc.scalar.activation(out=warm[:], in_=zero1[:], func=ACT.Sqrt, bias=1.0)
+        nc.scalar.activation(out=warm[:], in_=zero1[:], func=ACT.Abs_reciprocal_sqrt, bias=1.0)
         transposes(1)
         x_copy(1, "ss")
         nc.vector.tensor_copy(out=lam[:], in_=lam_bf[:])
         ve_scale(0)
         ve_scale(1)
 
-        for n in range(NPAIR):
-            matmuls(n)
+        for n in range(NPAIR + 1):
+            if n < NPAIR:
+                matmuls(n)
             if n + 2 < NPAIR:
                 transposes(n + 2)
+            if n >= 1:
+                products(n - 1)
             if n + 1 < NPAIR:
                 x_quant(n + 1)
-            v_blend(n)
-            if n >= 1:
-                rope(n - 1)
-                stores(n - 1)
-            sumsq(n)
+            if n < NPAIR:
+                sumsq(n)
+                scaled_tables(n)
             if n + 2 < NPAIR:
                 x_copy(n + 2, "ss")
                 ve_scale(n + 2)
-            normalise(n)
-        rope(NPAIR - 1)
-        stores(NPAIR - 1)
+            if n >= 1:
+                combine(n - 1)
+                passthrough(n - 1)
+            if n < NPAIR:
+                v_blend(n)
+            if n >= 1:
+                stores(n - 1)

@@ -264,12 +264,13 @@ def tile_causalselfattention_pa_t_kernel(tc, x, ve, qkv_w, lambdas, out_0, out_1
             b, j0 = where(n)
             rcs = work.tile([P, 8, 2, 32], F32, name="rcs")
             rcs_t[n] = rcs
-            nc.gpsimd.tensor_tensor(
-                out=rcs[:].rearrange("p (s q) t i -> p s q (t i)", s=2),
-                in0=cs[:, j0 : j0 + 2, :, :].rearrange("p j t i -> p j (t i)").unsqueeze(2).to_broadcast([P, 2, 4, 64]),
-                in1=r_t[n][:].rearrange("p (s q) -> p s q", s=2).unsqueeze(3).to_broadcast([P, 2, 4, 64]),
-                op=ALU.mult,
-            )
+            for s in range(2):
+                nc.gpsimd.tensor_tensor(
+                    out=rcs[:, 4 * s : 4 * s + 4, :, :].rearrange("p q t i -> p q (t i)"),
+                    in0=cs[:, j0 + s, :, :].rearrange("p t i -> p (t i)").unsqueeze(1).to_broadcast([P, 4, 64]),
+                    in1=r_t[n][:, 4 * s : 4 * s + 4].unsqueeze(2).to_broadcast([P, 4, 64]),
+                    op=ALU.mult,
+                )
 
         def products(n):
             t = work.tile([P, 2, 2, 2, H, 2, 32], F32, name="t")
@@ -289,6 +290,8 @@ def tile_causalselfattention_pa_t_kernel(tc, x, ve, qkv_w, lambdas, out_0, out_1
 
         def passthrough(n):
             b, j0 = where(n)
+            if j0 == 0:
+                qk_sb[b] = outp.tile([P, 2, J, HD], F32, name="qk_sb")
             for s in range(2):
                 nc.vector.tensor_tensor(
                     out=qk_sb[b][:, :, j0 + s, :].rearrange("p a (h z f) -> p a h z f", h=H, z=2)[:, :, :, :, 32:64],
@@ -303,8 +306,6 @@ def tile_causalselfattention_pa_t_kernel(tc, x, ve, qkv_w, lambdas, out_0, out_1
 
         def combine(n):
             b, j0 = where(n)
-            if j0 == 0:
-                qk_sb[b] = outp.tile([P, 2, J, HD], F32, name="qk_sb")
             y = qk_sb[b][:, :, j0 : j0 + 2, :].rearrange("p a j (h z f) -> p a (j h) z f", h=H, z=2)
             t = t_t[n][:].rearrange("p e a s h z i -> p e a (s h) z i")
             nc.vector.tensor_tensor(
@@ -344,26 +345,21 @@ def tile_causalselfattention_pa_t_kernel(tc, x, ve, qkv_w, lambdas, out_0, out_1
         nc.vector.tensor_copy(out=lam[:], in_=lam_bf[:])
         ve_scale(0)
         ve_scale(1)
+        x_quant(1)
 
-        for n in range(NPAIR + 1):
-            if n < NPAIR:
-                matmuls(n)
+        for n in range(NPAIR):
+            matmuls(n)
             if n + 2 < NPAIR:
                 transposes(n + 2)
-            if n >= 1:
-                products(n - 1)
-            if n + 1 < NPAIR:
-                x_quant(n + 1)
-            if n < NPAIR:
-                sumsq(n)
-                scaled_tables(n)
+            sumsq(n)
+            scaled_tables(n)
             if n + 2 < NPAIR:
                 x_copy(n + 2, "ss")
                 ve_scale(n + 2)
-            if n >= 1:
-                combine(n - 1)
-                passthrough(n - 1)
-            if n < NPAIR:
-                v_blend(n)
-            if n >= 1:
-                stores(n - 1)
+            passthrough(n)
+            v_blend(n)
+            products(n)
+            if n + 2 < NPAIR:
+                x_quant(n + 2)
+            combine(n)
+            stores(n)

@@ -23,7 +23,6 @@ NPAIR = B * J // 2
 EPS = 2.0 ** -23
 FLOPS = 2 * B * T * C * 3 * HD
 MANUAL = True
-VE_ON_SCALAR = (0, 1, 2, 3)
 
 
 def tile_causalselfattention_pa_t_kernel(tc, x, ve, qkv_w, lambdas, out_0, out_1, out_2):
@@ -228,10 +227,9 @@ def tile_causalselfattention_pa_t_kernel(tc, x, ve, qkv_w, lambdas, out_0, out_1
                 v_sb[b] = outp.tile([P, J, HD], F32, name="v_sb")
             dst = v_sb[b][:, j0 : j0 + 2, :]
             src = ve_sb[b][:, j0 : j0 + 2, :]
-            if n % 4 in VE_ON_SCALAR:
-                nc.scalar.activation(out=dst, in_=src, func=ACT.Copy, scale=lam[:, 1:2])
-            else:
-                nc.vector.tensor_scalar_mul(out=dst, in0=src, scalar1=lam[:, 1:2])
+            nc.gpsimd.tensor_scalar(
+                out=dst, in0=src, scalar1=lam[:, 1:2], scalar2=0.0, op0=ALU.mult, op1=ALU.add
+            )
 
         def v_blend(n):
             b, j0 = where(n)
@@ -288,21 +286,33 @@ def tile_causalselfattention_pa_t_kernel(tc, x, ve, qkv_w, lambdas, out_0, out_1
                         op=ALU.mult,
                     )
 
-        def passthrough(n):
+        def unrotated(n, s):
             b, j0 = where(n)
-            if j0 == 0:
-                qk_sb[b] = outp.tile([P, 2, J, HD], F32, name="qk_sb")
-            for s in range(2):
-                nc.vector.tensor_tensor(
-                    out=qk_sb[b][:, :, j0 + s, :].rearrange("p a (h z f) -> p a h z f", h=H, z=2)[:, :, :, :, 32:64],
-                    in0=qk_t[(n, s)][:].rearrange("p (a h z f) -> p a h z f", a=2, h=H, z=2)[:, :, :, :, 32:64],
-                    in1=r_t[n][:, 4 * s : 4 * s + 4]
-                    .rearrange("p (a h) -> p a h", a=2)
-                    .unsqueeze(3)
-                    .unsqueeze(4)
-                    .to_broadcast([P, 2, H, 2, 32]),
-                    op=ALU.mult,
-                )
+            out = qk_sb[b][:, :, j0 + s, :].rearrange("p a (h z f) -> p a h z f", h=H, z=2)[:, :, :, :, 32:64]
+            u = qk_t[(n, s)][:].rearrange("p (a h z f) -> p a h z f", a=2, h=H, z=2)[:, :, :, :, 32:64]
+            return out, u
+
+        def pass_scalar(n, s):
+            out, u = unrotated(n, s)
+            for a in range(2):
+                for h in range(H):
+                    q = 4 * s + 2 * a + h
+                    nc.scalar.activation(
+                        out=out[:, a, h, :, :], in_=u[:, a, h, :, :], func=ACT.Copy, scale=r_t[n][:, q : q + 1]
+                    )
+
+        def pass_vector(n, s):
+            out, u = unrotated(n, s)
+            nc.vector.tensor_tensor(
+                out=out,
+                in0=u,
+                in1=r_t[n][:, 4 * s : 4 * s + 4]
+                .rearrange("p (a h) -> p a h", a=2)
+                .unsqueeze(3)
+                .unsqueeze(4)
+                .to_broadcast([P, 2, H, 2, 32]),
+                op=ALU.mult,
+            )
 
         def combine(n):
             b, j0 = where(n)
@@ -348,15 +358,20 @@ def tile_causalselfattention_pa_t_kernel(tc, x, ve, qkv_w, lambdas, out_0, out_1
         x_quant(1)
 
         for n in range(NPAIR):
+            b, j0 = where(n)
+            if j0 == 0:
+                qk_sb[b] = outp.tile([P, 2, J, HD], F32, name="qk_sb")
             matmuls(n)
             if n + 2 < NPAIR:
                 transposes(n + 2)
             sumsq(n)
             scaled_tables(n)
             if n + 2 < NPAIR:
-                x_copy(n + 2, "ss")
                 ve_scale(n + 2)
-            passthrough(n)
+            pass_scalar(n, 1)
+            if n + 2 < NPAIR:
+                x_copy(n + 2, "ss")
+            pass_vector(n, 0)
             v_blend(n)
             products(n)
             if n + 2 < NPAIR:

@@ -153,7 +153,8 @@ def tile_causalselfattention_pa_t_kernel(tc, x, ve, qkv_w, lambdas, out_0, out_1
         xs_t = {}
         qk_t = {}
         v_t = {}
-        rcs_t = {}
+        ss_t = {}
+        junk_t = {}
         t_t = {}
         r_t = {}
         qk_sb = {}
@@ -162,25 +163,23 @@ def tile_causalselfattention_pa_t_kernel(tc, x, ve, qkv_w, lambdas, out_0, out_1
         def where(n):
             return n // 4, 2 * (n % 4)
 
-        def transposes(n):
+        def transposes(n, s):
             b, j0 = where(n)
             xw = x_sb[b][:].bitcast(F32)
-            for s in range(2):
-                xt = ps_xt.tile([P, 4, P], F32, name="xt", tag="xt")
-                for q in range(4):
-                    nc.tensor.transpose(xt[:, q, :], xw[:, j0 + s, (q // 2) * 256 + q % 2 : (q // 2 + 1) * 256 : 2], ident[:])
-                xt_t[(n, s)] = xt
+            xt = ps_xt.tile([P, 4, P], F32, name="xt", tag="xt")
+            for q in range(4):
+                nc.tensor.transpose(xt[:, q, :], xw[:, j0 + s, (q // 2) * 256 + q % 2 : (q // 2 + 1) * 256 : 2], ident[:])
+            xt_t[(n, s)] = xt
 
-        def x_copy(n, engs):
-            grp = work.tile([P, 2, 2, P, 4], BF16, name="grp", align_bytes=64)
-            grp_t[n] = grp
-            gf = grp[:].bitcast(F32)
-            for s in range(2):
-                src = xt_t[(n, s)][:].rearrange("p (g u) m -> p g m u", u=2)
-                if engs[s] == "s":
-                    nc.scalar.copy(out=gf[:, s, :, :, :], in_=src)
-                else:
-                    nc.vector.tensor_copy(out=gf[:, s, :, :, :], in_=src)
+        def x_copy(n, s, eng):
+            if s == 0:
+                grp_t[n] = work.tile([P, 2, 2, P, 4], BF16, name="grp", align_bytes=64)
+            dst = grp_t[n][:].bitcast(F32)[:, s, :, :, :]
+            src = xt_t[(n, s)][:].rearrange("p (g u) m -> p g m u", u=2)
+            if eng == "s":
+                nc.scalar.copy(out=dst, in_=src)
+            else:
+                nc.vector.tensor_copy(out=dst, in_=src)
 
         def x_quant(n):
             xc = work.tile([P, 2, 2, P], U32, name="xc", align_bytes=64)
@@ -193,24 +192,29 @@ def tile_causalselfattention_pa_t_kernel(tc, x, ve, qkv_w, lambdas, out_0, out_1
                 in_=grp_t[n][:].rearrange("p s g m t -> p (s g m t)"),
             )
 
-        def matmuls(n):
+        def matmul_qk(n, s):
+            xc = xc_t[n]
+            xs = xs_t[n]
+            qkps = ps_qk.tile([P, 2 * HD], F32, name="qkps", tag="qk")
+            qk_t[(n, s)] = qkps
+            for g in range(2):
+                nc.tensor.matmul_mx(
+                    out=qkps[:],
+                    lhsT=xc[:, s, g, :].bitcast(FP8X4),
+                    lhsT_scale=xs[:, s, g, :],
+                    rhs=wc[:, g, 0 : 2 * HD].bitcast(FP8X4),
+                    rhs_scale=ws[:, g, 0 : 2 * HD],
+                    start=(g == 0),
+                    stop=(g == 1),
+                )
+
+        def matmul_v(n):
             xc = xc_t[n]
             xs = xs_t[n]
             vps = ps_v.tile([P, 2, HD], F32, name="vps", tag="v")
             v_t[n] = vps
             for s in range(2):
-                qkps = ps_qk.tile([P, 2 * HD], F32, name="qkps", tag="qk")
-                qk_t[(n, s)] = qkps
                 for g in range(2):
-                    nc.tensor.matmul_mx(
-                        out=qkps[:],
-                        lhsT=xc[:, s, g, :].bitcast(FP8X4),
-                        lhsT_scale=xs[:, s, g, :],
-                        rhs=wc[:, g, 0 : 2 * HD].bitcast(FP8X4),
-                        rhs_scale=ws[:, g, 0 : 2 * HD],
-                        start=(g == 0),
-                        stop=(g == 1),
-                    )
                     nc.tensor.matmul_mx(
                         out=vps[:, s, :],
                         lhsT=xc[:, s, g, :].bitcast(FP8X4),
@@ -227,9 +231,7 @@ def tile_causalselfattention_pa_t_kernel(tc, x, ve, qkv_w, lambdas, out_0, out_1
                 v_sb[b] = outp.tile([P, J, HD], F32, name="v_sb")
             dst = v_sb[b][:, j0 : j0 + 2, :]
             src = ve_sb[b][:, j0 : j0 + 2, :]
-            nc.gpsimd.tensor_scalar(
-                out=dst, in0=src, scalar1=lam[:, 1:2], scalar2=0.0, op0=ALU.mult, op1=ALU.add
-            )
+            nc.vector.tensor_scalar_mul(out=dst, in0=src, scalar1=lam[:, 1:2])
 
         def v_blend(n):
             b, j0 = where(n)
@@ -243,76 +245,55 @@ def tile_causalselfattention_pa_t_kernel(tc, x, ve, qkv_w, lambdas, out_0, out_1
                 op1=ALU.add,
             )
 
-        def sumsq(n):
-            ss = small.tile([P, 8], F32, name="ss")
-            junk = work.tile([P, 8, D], BF16, name="junk")
-            for s in range(2):
-                for c in range(4):
-                    nc.scalar.activation(
-                        out=junk[:, 4 * s + c, :],
-                        in_=qk_t[(n, s)][:, c * D : (c + 1) * D],
-                        func=ACT.Square,
-                        accum_out=ss[:, 4 * s + c : 4 * s + c + 1],
-                    )
-            r = small.tile([P, 8], F32, name="r")
-            nc.scalar.activation(out=r[:], in_=ss[:], func=ACT.Abs_reciprocal_sqrt, scale=1.0 / D, bias=EPS)
-            r_t[n] = r
-
-        def scaled_tables(n):
-            b, j0 = where(n)
-            rcs = work.tile([P, 8, 2, 32], F32, name="rcs")
-            rcs_t[n] = rcs
-            for s in range(2):
-                nc.gpsimd.tensor_tensor(
-                    out=rcs[:, 4 * s : 4 * s + 4, :, :].rearrange("p q t i -> p q (t i)"),
-                    in0=cs[:, j0 + s, :, :].rearrange("p t i -> p (t i)").unsqueeze(1).to_broadcast([P, 4, 64]),
-                    in1=r_t[n][:, 4 * s : 4 * s + 4].unsqueeze(2).to_broadcast([P, 4, 64]),
-                    op=ALU.mult,
+        def sumsq(n, s):
+            if s == 0:
+                ss_t[n] = small.tile([P, 8], F32, name="ss")
+                r_t[n] = small.tile([P, 8], F32, name="r")
+                junk_t[n] = work.tile([P, 8, D], BF16, name="junk")
+            for q in range(4):
+                i = 4 * s + q
+                nc.scalar.activation(
+                    out=junk_t[n][:, i, :],
+                    in_=qk_t[(n, s)][:, q * D : (q + 1) * D],
+                    func=ACT.Square,
+                    accum_out=ss_t[n][:, i : i + 1],
                 )
 
-        def products(n):
-            t = work.tile([P, 2, 2, 2, H, 2, 32], F32, name="t")
-            t_t[n] = t
-            for s in range(2):
-                u = qk_t[(n, s)][:].rearrange("p (a h z f) -> p a h z f", a=2, h=H, z=2)[:, :, :, :, 0:32]
+        def rstd(n, s):
+            nc.scalar.activation(
+                out=r_t[n][:, 4 * s : 4 * s + 4],
+                in_=ss_t[n][:, 4 * s : 4 * s + 4],
+                func=ACT.Abs_reciprocal_sqrt,
+                scale=1.0 / D,
+                bias=EPS,
+            )
+
+        def products(n, s):
+            b, j0 = where(n)
+            if s == 0:
+                t_t[n] = work.tile([P, 2, 2, 2, H, 2, 32], F32, name="t")
+            u = qk_t[(n, s)][:].rearrange("p (q z f) -> p q z f", q=4, z=2)[:, :, :, 0:32]
+            for q in range(4):
                 for e in range(2):
-                    nc.vector.tensor_tensor(
-                        out=t[:, e, :, s, :, :, :],
-                        in0=u,
-                        in1=rcs_t[n][:, 4 * s : 4 * s + 4, e, :]
-                        .rearrange("p (a h) i -> p a h i", a=2)
-                        .unsqueeze(3)
-                        .to_broadcast([P, 2, H, 2, 32]),
-                        op=ALU.mult,
+                    nc.vector.scalar_tensor_tensor(
+                        out=t_t[n][:, e, q // 2, s, q % 2, :, :],
+                        in0=u[:, q, :, :],
+                        scalar=r_t[n][:, 4 * s + q : 4 * s + q + 1],
+                        in1=cs[:, j0 + s, e, :].unsqueeze(1).to_broadcast([P, 2, 32]),
+                        op0=ALU.mult,
+                        op1=ALU.mult,
                     )
 
         def unrotated(n, s):
             b, j0 = where(n)
             out = qk_sb[b][:, :, j0 + s, :].rearrange("p a (h z f) -> p a h z f", h=H, z=2)[:, :, :, :, 32:64]
             u = qk_t[(n, s)][:].rearrange("p (a h z f) -> p a h z f", a=2, h=H, z=2)[:, :, :, :, 32:64]
-            return out, u
-
-        def pass_scalar(n, s):
-            out, u = unrotated(n, s)
             for a in range(2):
                 for h in range(H):
                     q = 4 * s + 2 * a + h
                     nc.scalar.activation(
                         out=out[:, a, h, :, :], in_=u[:, a, h, :, :], func=ACT.Copy, scale=r_t[n][:, q : q + 1]
                     )
-
-        def pass_vector(n, s):
-            out, u = unrotated(n, s)
-            nc.vector.tensor_tensor(
-                out=out,
-                in0=u,
-                in1=r_t[n][:, 4 * s : 4 * s + 4]
-                .rearrange("p (a h) -> p a h", a=2)
-                .unsqueeze(3)
-                .unsqueeze(4)
-                .to_broadcast([P, 2, H, 2, 32]),
-                op=ALU.mult,
-            )
 
         def combine(n):
             b, j0 = where(n)
@@ -334,14 +315,16 @@ def tile_causalselfattention_pa_t_kernel(tc, x, ve, qkv_w, lambdas, out_0, out_1
                 nc.sync.dma_start(out=o_v[1][b][:, js, :], in_=qk_sb[b][:, 1, js, :])
 
         wts = [w_transpose(r) for r in range(4)]
-        transposes(0)
+        transposes(0, 0)
+        transposes(0, 1)
         wts.append(w_transpose(4))
         wts.append(w_transpose(5))
         w_copy(0, wts[0], "s")
         w_copy(1, wts[1], "v")
         w_copy(2, wts[2], "s")
         w_copy(3, wts[3], "v")
-        x_copy(0, "sv")
+        x_copy(0, 0, "s")
+        x_copy(0, 1, "v")
         w_quant(0, 0, 2 * HD)
         w_copy(4, wts[4], "s")
         w_copy(5, wts[5], "v")
@@ -350,31 +333,45 @@ def tile_causalselfattention_pa_t_kernel(tc, x, ve, qkv_w, lambdas, out_0, out_1
         w_quant(0, 2 * HD, 3 * HD)
         w_quant(1, 2 * HD, 3 * HD)
         nc.scalar.activation(out=warm[:], in_=zero1[:], func=ACT.Abs_reciprocal_sqrt, bias=1.0)
-        transposes(1)
-        x_copy(1, "ss")
+        transposes(1, 0)
+        transposes(1, 1)
+        x_copy(1, 0, "s")
+        x_copy(1, 1, "s")
         nc.vector.tensor_copy(out=lam[:], in_=lam_bf[:])
         ve_scale(0)
         ve_scale(1)
+        ve_scale(2)
         x_quant(1)
 
         for n in range(NPAIR):
             b, j0 = where(n)
             if j0 == 0:
                 qk_sb[b] = outp.tile([P, 2, J, HD], F32, name="qk_sb")
-            matmuls(n)
+            matmul_qk(n, 0)
+            matmul_qk(n, 1)
+            matmul_v(n)
             if n + 2 < NPAIR:
-                transposes(n + 2)
-            sumsq(n)
-            scaled_tables(n)
+                transposes(n + 2, 0)
+                transposes(n + 2, 1)
+            sumsq(n, 0)
+            sumsq(n, 1)
+            rstd(n, 0)
             if n + 2 < NPAIR:
-                ve_scale(n + 2)
-            pass_scalar(n, 1)
+                x_copy(n + 2, 0, "s")
+            rstd(n, 1)
+            unrotated(n, 0)
             if n + 2 < NPAIR:
-                x_copy(n + 2, "ss")
-            pass_vector(n, 0)
+                x_copy(n + 2, 1, "s")
+            unrotated(n, 1)
             v_blend(n)
-            products(n)
+            if n >= 1:
+                combine(n - 1)
+                stores(n - 1)
+            if n + 3 < NPAIR:
+                ve_scale(n + 3)
+            products(n, 0)
             if n + 2 < NPAIR:
                 x_quant(n + 2)
-            combine(n)
-            stores(n)
+            products(n, 1)
+        combine(NPAIR - 1)
+        stores(NPAIR - 1)

@@ -44,21 +44,22 @@ def tile_causalselfattention_pa_t_kernel(tc, x, ve, qkv_w, lambdas, out_0, out_1
         if MANUAL:
             ctx.enter_context(tc.manual_schedule())
 
+        tpos = const.tile([P, J], F32, name="tpos")
+        nc.gpsimd.iota(tpos[:], pattern=[[1, J]], base=0, channel_multiplier=J, allow_small_or_imprecise_dtypes=True)
         ident = const.tile([P, P], F32, name="ident")
         make_identity(nc, ident[:])
-        tpos_i = const.tile([P, J], I32, name="tpos_i")
-        nc.gpsimd.iota(tpos_i[:], pattern=[[1, J]], base=0, channel_multiplier=J)
+        perm = const.tile([P, P], F32, name="perm")
 
         lam_bf = const.tile([P, 2], BF16, name="lam_bf")
-        nc.scalar.dma_start(out=lam_bf[:], in_=lambdas.partition_broadcast(P))
         w_sb = const.tile([P, 6, C], BF16, name="w_sb")
         x_sb = [xin.tile([P, J, C], BF16, name="x_sb") for b in range(B)]
         ve_sb = [xin.tile([P, J, HD], BF16, name="ve_sb") for b in range(B)]
-        nc.sync.dma_start(out=w_sb[:, 0:2, :], in_=w_v[:, 0:2, :])
-        nc.sync.dma_start(out=w_sb[:, 2:4, :], in_=w_v[:, 2:4, :])
+        for r in range(4):
+            nc.sync.dma_start(out=w_sb[:, r, :], in_=w_v[:, r, :])
         nc.sync.dma_start(out=x_sb[0][:, 0:2, :], in_=x_v[0][:, 0:2, :])
         nc.sync.dma_start(out=w_sb[:, 4:6, :], in_=w_v[:, 4:6, :])
         nc.sync.dma_start(out=x_sb[0][:, 2:4, :], in_=x_v[0][:, 2:4, :])
+        nc.sync.dma_start(out=lam_bf[:], in_=lambdas.partition_broadcast(P))
         nc.sync.dma_start(out=ve_sb[0][:], in_=ve_v[0])
         nc.sync.dma_start(out=x_sb[0][:, 4:8, :], in_=x_v[0][:, 4:8, :])
         for b in range(1, B):
@@ -75,45 +76,47 @@ def tile_causalselfattention_pa_t_kernel(tc, x, ve, qkv_w, lambdas, out_0, out_1
         for i in range(8):
             nc.vector.tensor_scalar_add(out=turns[:, i : i + 1], in0=zero1[:], scalar1=ratio ** i / (2.0 * math.pi))
         nc.vector.tensor_scalar_mul(out=turns[:, 8:16], in0=turns[:, 0:8], scalar1=ratio ** 8)
+        nc.vector.tensor_copy(
+            out=perm[:].rearrange("p (y z i) -> p y z i", y=2, z=2),
+            in_=ident[:].rearrange("p (z y i) -> p y z i", y=2, z=2),
+        )
         nc.vector.tensor_scalar_mul(out=turns[:, 16:32], in0=turns[:, 0:16], scalar1=ratio ** 16)
-        tpos = const.tile([P, J], F32, name="tpos")
-        nc.vector.tensor_copy(out=tpos[:], in_=tpos_i[:])
         ang = const.tile([P, J, 32], F32, name="ang")
-        nc.vector.tensor_tensor(
-            out=ang[:],
-            in0=tpos[:].unsqueeze(2).to_broadcast([P, J, 32]),
-            in1=turns[:].unsqueeze(1).to_broadcast([P, J, 32]),
-            op=ALU.mult,
-        )
-        whole_i = const.tile([P, J, 32], I32, name="whole_i")
-        nc.vector.tensor_copy(out=whole_i[:], in_=ang[:])
-        whole = const.tile([P, J, 32], F32, name="whole")
-        nc.vector.tensor_copy(out=whole[:], in_=whole_i[:])
-        frac = const.tile([P, J * 32], F32, name="frac")
-        nc.vector.tensor_sub(
-            out=frac[:], in0=ang[:].rearrange("p j i -> p (j i)"), in1=whole[:].rearrange("p j i -> p (j i)")
-        )
-        negf = const.tile([P, J * 32], F32, name="negf")
-        nc.vector.scalar_tensor_tensor(
-            out=negf[:], in0=frac[:], scalar=0.5, in1=frac[:], op0=ALU.is_gt, op1=ALU.subtract
-        )
-        absf = const.tile([P, J * 32], F32, name="absf")
-        nc.vector.scalar_tensor_tensor(
-            out=absf[:], in0=negf[:], scalar=-1.0, in1=negf[:], op0=ALU.mult, op1=ALU.max
-        )
-        cs = const.tile([P, J, 2, 32], F32, name="cs")
+        whole = const.tile([P, J, 32], I32, name="whole")
+        negf = const.tile([P, J, 32], F32, name="negf")
+        absf = const.tile([P, J, 32], F32, name="absf")
+        halves = [slice(0, J // 2), slice(J // 2, J)]
+        for js in halves:
+            nc.vector.tensor_tensor(
+                out=ang[:, js, :],
+                in0=tpos[:, js].unsqueeze(2).to_broadcast([P, J // 2, 32]),
+                in1=turns[:].unsqueeze(1).to_broadcast([P, J // 2, 32]),
+                op=ALU.mult,
+            )
+        for js in halves:
+            nc.vector.tensor_copy(out=whole[:, js, :], in_=ang[:, js, :])
+        for js in halves:
+            nc.vector.tensor_tensor(out=negf[:, js, :], in0=whole[:, js, :], in1=ang[:, js, :], op=ALU.subtract)
+        for js in halves:
+            nc.vector.scalar_tensor_tensor(
+                out=absf[:, js, :].rearrange("p j i -> p (j i)"),
+                in0=negf[:, js, :].rearrange("p j i -> p (j i)"),
+                scalar=-1.0,
+                in1=negf[:, js, :].rearrange("p j i -> p (j i)"),
+                op0=ALU.mult,
+                op1=ALU.max,
+            )
+        cs = const.tile([P, J, 2, 2, 32], F32, name="cs")
+        nc.scalar.activation(out=cs[:, :, 1, 0, :], in_=negf[:], func=ACT.Sin, scale=2.0 * math.pi)
         nc.scalar.activation(
-            out=cs[:, :, 0, :],
-            in_=absf[:].rearrange("p (j i) -> p j i", j=J),
-            func=ACT.Sin,
-            scale=-2.0 * math.pi,
-            bias=0.5 * math.pi,
+            out=cs[:, :, 0, 0, :], in_=absf[:], func=ACT.Sin, scale=-2.0 * math.pi, bias=0.5 * math.pi
         )
-        nc.scalar.activation(
-            out=cs[:, :, 1, :],
-            in_=negf[:].rearrange("p (j i) -> p j i", j=J),
-            func=ACT.Sin,
-            scale=-2.0 * math.pi,
+        nc.scalar.activation(out=warm[:], in_=zero1[:], func=ACT.Abs_reciprocal_sqrt, bias=1.0)
+        nc.gpsimd.tensor_scalar(
+            out=cs[:, :, 1, 1, :], in0=cs[:, :, 1, 0, :], scalar1=-1.0, scalar2=0.0, op0=ALU.mult, op1=ALU.add
+        )
+        nc.gpsimd.tensor_scalar(
+            out=cs[:, :, 0, 1, :], in0=cs[:, :, 0, 0, :], scalar1=1.0, scalar2=0.0, op0=ALU.mult, op1=ALU.add
         )
         lam = const.tile([P, 2], F32, name="lam")
 
@@ -128,8 +131,9 @@ def tile_causalselfattention_pa_t_kernel(tc, x, ve, qkv_w, lambdas, out_0, out_1
                 wt = ps_qk.tile([P, 4, P], F32, name="wt", tag="qk")
             else:
                 wt = ps_v.tile([P, 4, P], F32, name="wt", tag="v")
+            order = perm if r < 4 else ident
             for q in range(4):
-                nc.tensor.transpose(wt[:, q, :], w_words[:, r, (q // 2) * 256 + q % 2 : (q // 2 + 1) * 256 : 2], ident[:])
+                nc.tensor.transpose(wt[:, q, :], w_words[:, r, (q // 2) * 256 + q % 2 : (q // 2 + 1) * 256 : 2], order[:])
             return wt
 
         def w_copy(r, wt, eng):
@@ -181,15 +185,14 @@ def tile_causalselfattention_pa_t_kernel(tc, x, ve, qkv_w, lambdas, out_0, out_1
             else:
                 nc.vector.tensor_copy(out=dst, in_=src)
 
-        def x_quant(n):
-            xc = work.tile([P, 2, 2, P], U32, name="xc", align_bytes=64)
-            xs = work.tile([P, 2, 2, P], U8, name="xs", align_bytes=64)
-            xc_t[n] = xc
-            xs_t[n] = xs
+        def x_quant(n, s0=0, s1=2):
+            if s0 == 0:
+                xc_t[n] = work.tile([P, 2, 2, P], U32, name="xc", align_bytes=64)
+                xs_t[n] = work.tile([P, 2, 2, P], U8, name="xs", align_bytes=64)
             nc.vector.quantize_mx(
-                out=xc[:].rearrange("p s g m -> p (s g m)").bitcast(FP8X4),
-                scales=xs[:].rearrange("p s g m -> p (s g m)"),
-                in_=grp_t[n][:].rearrange("p s g m t -> p (s g m t)"),
+                out=xc_t[n][:, s0:s1, :, :].rearrange("p s g m -> p (s g m)").bitcast(FP8X4),
+                scales=xs_t[n][:, s0:s1, :, :].rearrange("p s g m -> p (s g m)"),
+                in_=grp_t[n][:, s0:s1, :, :, :].rearrange("p s g m t -> p (s g m t)"),
             )
 
         def matmul_qk(n, s):
@@ -271,23 +274,21 @@ def tile_causalselfattention_pa_t_kernel(tc, x, ve, qkv_w, lambdas, out_0, out_1
         def products(n, s):
             b, j0 = where(n)
             if s == 0:
-                t_t[n] = work.tile([P, 2, 2, 2, H, 2, 32], F32, name="t")
-            u = qk_t[(n, s)][:].rearrange("p (q z f) -> p q z f", q=4, z=2)[:, :, :, 0:32]
+                t_t[n] = work.tile([P, 2, 2, 2, H, D // 2], F32, name="t")
             for q in range(4):
-                for e in range(2):
-                    nc.vector.scalar_tensor_tensor(
-                        out=t_t[n][:, e, q // 2, s, q % 2, :, :],
-                        in0=u[:, q, :, :],
-                        scalar=r_t[n][:, 4 * s + q : 4 * s + q + 1],
-                        in1=cs[:, j0 + s, e, :].unsqueeze(1).to_broadcast([P, 2, 32]),
-                        op0=ALU.mult,
-                        op1=ALU.mult,
-                    )
+                nc.vector.scalar_tensor_tensor(
+                    out=t_t[n][:, :, q // 2, s, q % 2, :],
+                    in0=qk_t[(n, s)][:, q * D : q * D + D // 2].unsqueeze(1).to_broadcast([P, 2, D // 2]),
+                    scalar=r_t[n][:, 4 * s + q : 4 * s + q + 1],
+                    in1=cs[:, j0 + s, :, :, :].rearrange("p e z i -> p e (z i)"),
+                    op0=ALU.mult,
+                    op1=ALU.mult,
+                )
 
         def unrotated(n, s):
             b, j0 = where(n)
             out = qk_sb[b][:, :, j0 + s, :].rearrange("p a (h z f) -> p a h z f", h=H, z=2)[:, :, :, :, 32:64]
-            u = qk_t[(n, s)][:].rearrange("p (a h z f) -> p a h z f", a=2, h=H, z=2)[:, :, :, :, 32:64]
+            u = qk_t[(n, s)][:].rearrange("p (a h y z i) -> p a h y z i", a=2, h=H, y=2, z=2)[:, :, :, 1, :, :]
             for a in range(2):
                 for h in range(H):
                     q = 4 * s + 2 * a + h
@@ -298,50 +299,49 @@ def tile_causalselfattention_pa_t_kernel(tc, x, ve, qkv_w, lambdas, out_0, out_1
         def combine(n):
             b, j0 = where(n)
             y = qk_sb[b][:, :, j0 : j0 + 2, :].rearrange("p a j (h z f) -> p a (j h) z f", h=H, z=2)
-            t = t_t[n][:].rearrange("p e a s h z i -> p e a (s h) z i")
-            nc.vector.tensor_tensor(
-                out=y[:, :, :, 0, 0:32], in0=t[:, 0, :, :, 0, :], in1=t[:, 1, :, :, 1, :], op=ALU.add
-            )
-            nc.vector.tensor_tensor(
-                out=y[:, :, :, 1, 0:32], in0=t[:, 0, :, :, 1, :], in1=t[:, 1, :, :, 0, :], op=ALU.subtract
-            )
+            t = t_t[n][:].rearrange("p e a s h (z i) -> p e a (s h) z i", z=2)
+            for z in range(2):
+                nc.gpsimd.tensor_tensor(
+                    out=y[:, :, :, z, 0:32], in0=t[:, 0, :, :, z, :], in1=t[:, 1, :, :, 1 - z, :], op=ALU.add
+                )
 
-        def stores(n):
+        def combine_tile(n, s):
             b, j0 = where(n)
-            if j0 % 4 == 2:
-                js = slice(j0 - 2, j0 + 2)
-                nc.sync.dma_start(out=o_v[2][b][:, js, :], in_=v_sb[b][:, js, :])
-                nc.sync.dma_start(out=o_v[0][b][:, js, :], in_=qk_sb[b][:, 0, js, :])
-                nc.sync.dma_start(out=o_v[1][b][:, js, :], in_=qk_sb[b][:, 1, js, :])
+            y = qk_sb[b][:, :, j0 + s, :].rearrange("p a (h z f) -> p a h z f", h=H, z=2)
+            t = t_t[n][:, :, :, s, :, :].rearrange("p e a h (z i) -> p e a h z i", z=2)
+            for z in range(2):
+                nc.vector.tensor_tensor(
+                    out=y[:, :, :, z, 0:32], in0=t[:, 0, :, :, z, :], in1=t[:, 1, :, :, 1 - z, :], op=ALU.add
+                )
+
+        def store_qk(b, js):
+            nc.sync.dma_start(out=o_v[0][b][:, js, :], in_=qk_sb[b][:, 0, js, :])
+            nc.sync.dma_start(out=o_v[1][b][:, js, :], in_=qk_sb[b][:, 1, js, :])
+
+        def store_v(b, js):
+            nc.sync.dma_start(out=o_v[2][b][:, js, :], in_=v_sb[b][:, js, :])
 
         wts = [w_transpose(r) for r in range(4)]
         transposes(0, 0)
         transposes(0, 1)
         wts.append(w_transpose(4))
         wts.append(w_transpose(5))
-        w_copy(0, wts[0], "s")
-        w_copy(1, wts[1], "v")
-        w_copy(2, wts[2], "s")
-        w_copy(3, wts[3], "v")
+        w_copy(0, wts[0], "v")
+        w_copy(1, wts[1], "s")
+        w_copy(2, wts[2], "v")
+        w_copy(3, wts[3], "s")
+        w_quant(0, 0, HD)
+        w_quant(1, 0, HD)
         x_copy(0, 0, "s")
-        x_copy(0, 1, "v")
-        w_quant(0, 0, 2 * HD)
-        w_copy(4, wts[4], "s")
-        w_copy(5, wts[5], "v")
-        w_quant(1, 0, 2 * HD)
-        x_quant(0)
+        w_quant(0, HD, 2 * HD)
+        w_quant(1, HD, 2 * HD)
+        x_quant(0, 0, 1)
+        x_copy(0, 1, "s")
+        w_copy(4, wts[4], "v")
+        x_quant(0, 1, 2)
+        w_copy(5, wts[5], "s")
         w_quant(0, 2 * HD, 3 * HD)
         w_quant(1, 2 * HD, 3 * HD)
-        nc.scalar.activation(out=warm[:], in_=zero1[:], func=ACT.Abs_reciprocal_sqrt, bias=1.0)
-        transposes(1, 0)
-        transposes(1, 1)
-        x_copy(1, 0, "s")
-        x_copy(1, 1, "s")
-        nc.vector.tensor_copy(out=lam[:], in_=lam_bf[:])
-        ve_scale(0)
-        ve_scale(1)
-        ve_scale(2)
-        x_quant(1)
 
         for n in range(NPAIR):
             b, j0 = where(n)
@@ -349,29 +349,59 @@ def tile_causalselfattention_pa_t_kernel(tc, x, ve, qkv_w, lambdas, out_0, out_1
                 qk_sb[b] = outp.tile([P, 2, J, HD], F32, name="qk_sb")
             matmul_qk(n, 0)
             matmul_qk(n, 1)
+            if n == 0:
+                transposes(1, 0)
+                transposes(1, 1)
+                x_copy(1, 0, "v")
+                x_copy(1, 1, "v")
             matmul_v(n)
             if n + 2 < NPAIR:
                 transposes(n + 2, 0)
                 transposes(n + 2, 1)
+            if n == 0:
+                nc.vector.tensor_copy(out=lam[:], in_=lam_bf[:])
+                ve_scale(0)
+                x_quant(1)
+                ve_scale(1)
+                ve_scale(2)
             sumsq(n, 0)
             sumsq(n, 1)
             rstd(n, 0)
             if n + 2 < NPAIR:
                 x_copy(n + 2, 0, "s")
             rstd(n, 1)
+            if n == NPAIR - 1:
+                break
             unrotated(n, 0)
-            if n + 2 < NPAIR:
+            if n + 2 < NPAIR and n % 2 == 0:
                 x_copy(n + 2, 1, "s")
             unrotated(n, 1)
-            v_blend(n)
-            if n >= 1:
-                combine(n - 1)
-                stores(n - 1)
             if n + 3 < NPAIR:
                 ve_scale(n + 3)
+            v_blend(n)
+            if n + 2 < NPAIR and n % 2 == 1:
+                x_copy(n + 2, 1, "v")
             products(n, 0)
             if n + 2 < NPAIR:
                 x_quant(n + 2)
             products(n, 1)
-        combine(NPAIR - 1)
-        stores(NPAIR - 1)
+            combine(n)
+            if j0 % 4 == 2:
+                store_v(b, slice(j0 - 2, j0 + 2))
+                store_qk(b, slice(j0 - 2, j0 + 2))
+
+        last = NPAIR - 1
+        b, j0 = where(last)
+        before = slice(j0 - 2, j0)
+        own = slice(j0, j0 + 2)
+        store_v(b, before)
+        store_qk(b, before)
+        products(last, 0)
+        unrotated(last, 0)
+        v_blend(last)
+        store_v(b, own)
+        combine_tile(last, 0)
+        products(last, 1)
+        unrotated(last, 1)
+        combine_tile(last, 1)
+        store_qk(b, own)

@@ -232,9 +232,15 @@ def tile_causalselfattention_pa_t_kernel(tc, x, ve, qkv_w, lambdas, out_0, out_1
             b, j0 = where(n)
             if j0 == 0:
                 v_sb[b] = outp.tile([P, J, HD], F32, name="v_sb")
-            dst = v_sb[b][:, j0 : j0 + 2, :]
-            src = ve_sb[b][:, j0 : j0 + 2, :]
-            nc.vector.tensor_scalar_mul(out=dst, in0=src, scalar1=lam[:, 1:2])
+            for s in range(2):
+                nc.gpsimd.tensor_scalar(
+                    out=v_sb[b][:, j0 + s, :],
+                    in0=ve_sb[b][:, j0 + s, :],
+                    scalar1=lam[:, 1:2],
+                    scalar2=0.0,
+                    op0=ALU.mult,
+                    op1=ALU.add,
+                )
 
         def v_blend(n):
             b, j0 = where(n)
@@ -305,12 +311,12 @@ def tile_causalselfattention_pa_t_kernel(tc, x, ve, qkv_w, lambdas, out_0, out_1
                     out=y[:, :, :, z, 0:32], in0=t[:, 0, :, :, z, :], in1=t[:, 1, :, :, 1 - z, :], op=ALU.add
                 )
 
-        def combine_tile(n, s):
+        def combine_tile(n, s, eng):
             b, j0 = where(n)
             y = qk_sb[b][:, :, j0 + s, :].rearrange("p a (h z f) -> p a h z f", h=H, z=2)
             t = t_t[n][:, :, :, s, :, :].rearrange("p e a h (z i) -> p e a h z i", z=2)
             for z in range(2):
-                nc.vector.tensor_tensor(
+                eng.tensor_tensor(
                     out=y[:, :, :, z, 0:32], in0=t[:, 0, :, :, z, :], in1=t[:, 1, :, :, 1 - z, :], op=ALU.add
                 )
 
@@ -373,19 +379,17 @@ def tile_causalselfattention_pa_t_kernel(tc, x, ve, qkv_w, lambdas, out_0, out_1
             if n == NPAIR - 1:
                 break
             unrotated(n, 0)
-            if n + 2 < NPAIR and n % 2 == 0:
-                x_copy(n + 2, 1, "s")
             unrotated(n, 1)
-            if n + 3 < NPAIR:
-                ve_scale(n + 3)
             v_blend(n)
-            if n + 2 < NPAIR and n % 2 == 1:
+            if n + 2 < NPAIR:
                 x_copy(n + 2, 1, "v")
             products(n, 0)
             if n + 2 < NPAIR:
                 x_quant(n + 2)
             products(n, 1)
             combine(n)
+            if n + 3 < NPAIR:
+                ve_scale(n + 3)
             if j0 % 4 == 2:
                 store_v(b, slice(j0 - 2, j0 + 2))
                 store_qk(b, slice(j0 - 2, j0 + 2))
@@ -396,12 +400,16 @@ def tile_causalselfattention_pa_t_kernel(tc, x, ve, qkv_w, lambdas, out_0, out_1
         own = slice(j0, j0 + 2)
         store_v(b, before)
         store_qk(b, before)
+        v_raw = work.tile([P, 2, HD], F32, name="v_raw")
+        nc.scalar.activation(out=v_raw[:], in_=v_t[last][:], func=ACT.Copy, scale=lam[:, 0:1])
         products(last, 0)
         unrotated(last, 0)
-        v_blend(last)
-        store_v(b, own)
-        combine_tile(last, 0)
         products(last, 1)
         unrotated(last, 1)
-        combine_tile(last, 1)
+        combine_tile(last, 0, nc.gpsimd)
+        nc.vector.tensor_tensor(
+            out=v_sb[b][:, own, :], in0=v_raw[:], in1=v_sb[b][:, own, :], op=ALU.add
+        )
+        combine_tile(last, 1, nc.vector)
+        store_v(b, own)
         store_qk(b, own)

@@ -56,12 +56,14 @@ def tile_causalselfattention_pa_t_kernel(tc, x, ve, qkv_w, lambdas, out_0, out_1
         ve_sb = [xin.tile([P, J, HD], BF16, name="ve_sb") for b in range(B)]
         for r in range(4):
             nc.sync.dma_start(out=w_sb[:, r, :], in_=w_v[:, r, :])
-        nc.sync.dma_start(out=x_sb[0][:, 0:2, :], in_=x_v[0][:, 0:2, :])
+        nc.sync.dma_start(out=x_sb[0][:, 0, :], in_=x_v[0][:, 0, :])
+        nc.sync.dma_start(out=x_sb[0][:, 1, :], in_=x_v[0][:, 1, :])
         nc.sync.dma_start(out=w_sb[:, 4:6, :], in_=w_v[:, 4:6, :])
         nc.sync.dma_start(out=x_sb[0][:, 2:4, :], in_=x_v[0][:, 2:4, :])
+        nc.sync.dma_start(out=x_sb[0][:, 4:6, :], in_=x_v[0][:, 4:6, :])
         nc.sync.dma_start(out=lam_bf[:], in_=lambdas.partition_broadcast(P))
         nc.sync.dma_start(out=ve_sb[0][:], in_=ve_v[0])
-        nc.sync.dma_start(out=x_sb[0][:, 4:8, :], in_=x_v[0][:, 4:8, :])
+        nc.sync.dma_start(out=x_sb[0][:, 6:8, :], in_=x_v[0][:, 6:8, :])
         for b in range(1, B):
             nc.sync.dma_start(out=x_sb[b][:, 0:4, :], in_=x_v[b][:, 0:4, :])
             nc.sync.dma_start(out=ve_sb[b][:], in_=ve_v[b])
@@ -346,8 +348,16 @@ def tile_causalselfattention_pa_t_kernel(tc, x, ve, qkv_w, lambdas, out_0, out_1
         w_copy(4, wts[4], "v")
         x_quant(0, 1, 2)
         w_copy(5, wts[5], "s")
+        transposes(1, 0)
+        transposes(1, 1)
         w_quant(0, 2 * HD, 3 * HD)
         w_quant(1, 2 * HD, 3 * HD)
+        x_copy(1, 0, "s")
+        x_copy(1, 1, "v")
+        nc.vector.tensor_copy(out=lam[:], in_=lam_bf[:])
+        x_quant(1)
+        for n in range(3):
+            ve_scale(n)
 
         for n in range(NPAIR):
             b, j0 = where(n)
@@ -355,21 +365,10 @@ def tile_causalselfattention_pa_t_kernel(tc, x, ve, qkv_w, lambdas, out_0, out_1
                 qk_sb[b] = outp.tile([P, 2, J, HD], F32, name="qk_sb")
             matmul_qk(n, 0)
             matmul_qk(n, 1)
-            if n == 0:
-                transposes(1, 0)
-                transposes(1, 1)
-                x_copy(1, 0, "v")
-                x_copy(1, 1, "v")
-            matmul_v(n)
             if n + 2 < NPAIR:
                 transposes(n + 2, 0)
                 transposes(n + 2, 1)
-            if n == 0:
-                nc.vector.tensor_copy(out=lam[:], in_=lam_bf[:])
-                ve_scale(0)
-                x_quant(1)
-                ve_scale(1)
-                ve_scale(2)
+            matmul_v(n)
             sumsq(n, 0)
             sumsq(n, 1)
             rstd(n, 0)
@@ -378,15 +377,15 @@ def tile_causalselfattention_pa_t_kernel(tc, x, ve, qkv_w, lambdas, out_0, out_1
             rstd(n, 1)
             if n == NPAIR - 1:
                 break
-            unrotated(n, 0)
-            unrotated(n, 1)
-            v_blend(n)
             if n + 2 < NPAIR:
                 x_copy(n + 2, 1, "v")
+            unrotated(n, 0)
+            unrotated(n, 1)
             products(n, 0)
+            products(n, 1)
             if n + 2 < NPAIR:
                 x_quant(n + 2)
-            products(n, 1)
+            v_blend(n)
             combine(n)
             if n + 3 < NPAIR:
                 ve_scale(n + 3)
@@ -410,6 +409,7 @@ def tile_causalselfattention_pa_t_kernel(tc, x, ve, qkv_w, lambdas, out_0, out_1
         nc.vector.tensor_tensor(
             out=v_sb[b][:, own, :], in0=v_raw[:], in1=v_sb[b][:, own, :], op=ALU.add
         )
-        combine_tile(last, 1, nc.vector)
         store_v(b, own)
-        store_qk(b, own)
+        store_qk(b, slice(j0, j0 + 1))
+        combine_tile(last, 1, nc.vector)
+        store_qk(b, slice(j0 + 1, j0 + 2))

@@ -124,8 +124,8 @@ def tile_causalselfattention_pa_t_kernel(tc, x, ve, qkv_w, lambdas, out_0, out_1
 
         wg = const.tile([P, 2, 3 * HD, 4], BF16, name="wg", align_bytes=64)
         wgf = wg[:].bitcast(F32)
-        wc = const.tile([P, 2, 3 * HD], U32, name="wc", align_bytes=64)
-        ws = const.tile([P, 2, 3 * HD], U8, name="ws", align_bytes=64)
+        wc = const.tile([P, 2, 3 * HD], U32, name="wc", align_bytes=256)
+        ws = const.tile([P, 2, 3 * HD], U8, name="ws", align_bytes=256)
         w_words = w_sb[:].bitcast(F32)
 
         def w_transpose(r):
@@ -189,8 +189,8 @@ def tile_causalselfattention_pa_t_kernel(tc, x, ve, qkv_w, lambdas, out_0, out_1
 
         def x_quant(n, s0=0, s1=2):
             if s0 == 0:
-                xc_t[n] = work.tile([P, 2, 2, P], U32, name="xc", align_bytes=64)
-                xs_t[n] = work.tile([P, 2, 2, P], U8, name="xs", align_bytes=64)
+                xc_t[n] = work.tile([P, 2, 2, P], U32, name="xc", align_bytes=256)
+                xs_t[n] = work.tile([P, 2, 2, P], U8, name="xs", align_bytes=256)
             nc.vector.quantize_mx(
                 out=xc_t[n][:, s0:s1, :, :].rearrange("p s g m -> p (s g m)").bitcast(FP8X4),
                 scales=xs_t[n][:, s0:s1, :, :].rearrange("p s g m -> p (s g m)"),

@@ -54,7 +54,9 @@ def tile_causalselfattention_pa_t_kernel(tc, x, ve, qkv_w, lambdas, out_0, out_1
         w_sb = const.tile([P, 6, C], BF16, name="w_sb")
         x_sb = [xin.tile([P, J, C], BF16, name="x_sb") for b in range(B)]
         ve_sb = [xin.tile([P, J, HD], BF16, name="ve_sb") for b in range(B)]
-        for r in range(4):
+        for c0 in (0, C // 2):
+            nc.sync.dma_start(out=w_sb[:, 0, c0 : c0 + C // 2], in_=w_v[:, 0, c0 : c0 + C // 2])
+        for r in range(1, 4):
             nc.sync.dma_start(out=w_sb[:, r, :], in_=w_v[:, r, :])
         nc.sync.dma_start(out=x_sb[0][:, 0, :], in_=x_v[0][:, 0, :])
         nc.sync.dma_start(out=x_sb[0][:, 1, :], in_=x_v[0][:, 1, :])
@@ -304,12 +306,12 @@ def tile_causalselfattention_pa_t_kernel(tc, x, ve, qkv_w, lambdas, out_0, out_1
                         out=out[:, a, h, :, :], in_=u[:, a, h, :, :], func=ACT.Copy, scale=r_t[n][:, q : q + 1]
                     )
 
-        def combine(n):
+        def combine(n, engines):
             b, j0 = where(n)
             y = qk_sb[b][:, :, j0 : j0 + 2, :].rearrange("p a j (h z f) -> p a (j h) z f", h=H, z=2)
             t = t_t[n][:].rearrange("p e a s h (z i) -> p e a (s h) z i", z=2)
             for z in range(2):
-                nc.gpsimd.tensor_tensor(
+                engines[z].tensor_tensor(
                     out=y[:, :, :, z, 0:32], in0=t[:, 0, :, :, z, :], in1=t[:, 1, :, :, 1 - z, :], op=ALU.add
                 )
 
@@ -386,30 +388,27 @@ def tile_causalselfattention_pa_t_kernel(tc, x, ve, qkv_w, lambdas, out_0, out_1
             if n + 2 < NPAIR:
                 x_quant(n + 2)
             v_blend(n)
-            combine(n)
+            combine(n, (nc.gpsimd, nc.vector if n == NPAIR - 2 else nc.gpsimd))
             if n + 3 < NPAIR:
                 ve_scale(n + 3)
-            if j0 % 4 == 2:
-                store_v(b, slice(j0 - 2, j0 + 2))
-                store_qk(b, slice(j0 - 2, j0 + 2))
+            if n < NPAIR - 4:
+                if j0 % 4 == 2:
+                    store_v(b, slice(j0 - 2, j0 + 2))
+                    store_qk(b, slice(j0 - 2, j0 + 2))
+            else:
+                store_v(b, slice(j0, j0 + 2))
+                store_qk(b, slice(j0, j0 + 2))
 
         last = NPAIR - 1
         b, j0 = where(last)
-        before = slice(j0 - 2, j0)
         own = slice(j0, j0 + 2)
-        store_v(b, before)
-        store_qk(b, before)
-        v_raw = work.tile([P, 2, HD], F32, name="v_raw")
-        nc.scalar.activation(out=v_raw[:], in_=v_t[last][:], func=ACT.Copy, scale=lam[:, 0:1])
+        v_blend(last)
+        store_v(b, own)
         products(last, 0)
         unrotated(last, 0)
         products(last, 1)
         unrotated(last, 1)
-        combine_tile(last, 0, nc.gpsimd)
-        nc.vector.tensor_tensor(
-            out=v_sb[b][:, own, :], in0=v_raw[:], in1=v_sb[b][:, own, :], op=ALU.add
-        )
-        store_v(b, own)
+        combine_tile(last, 0, nc.vector)
         store_qk(b, slice(j0, j0 + 1))
         combine_tile(last, 1, nc.vector)
         store_qk(b, slice(j0 + 1, j0 + 2))

import math
from contextlib import ExitStack

import concourse.bass as bass
import concourse.mybir as mybir
import concourse.tile as tile
from concourse.masks import make_identity

F32 = mybir.dt.float32
BF16 = mybir.dt.bfloat16
I32 = mybir.dt.int32
U32 = mybir.dt.uint32
U8 = mybir.dt.uint8
FP8X4 = mybir.dt.float8_e4m3fn_x4
ALU = mybir.AluOpType
ACT = mybir.ActivationFunctionType

B, T, C, H, D = 4, 1024, 1024, 2, 128
HD = H * D
P = 128
J = T // P
NPAIR = B * J // 2
EPS = 2.0 ** -23
FLOPS = 2 * B * T * C * 3 * HD
MANUAL = True


def tile_causalselfattention_pa_t_kernel(tc, x, ve, qkv_w, lambdas, out_0, out_1, out_2):
    nc = tc.nc
    x_v = x.rearrange("b (p j) c -> b p j c", j=J)
    ve_v = ve.rearrange("b (p j) f -> b p j f", j=J)
    w_v = qkv_w.rearrange("s (r p) c -> p (s r) c", p=P)
    o_v = [o.rearrange("b (p j) h d -> b p j (h d)", j=J) for o in (out_0, out_1, out_2)]

    with ExitStack() as ctx:
        const = ctx.enter_context(tc.tile_pool(name="const", bufs=1))
        xin = ctx.enter_context(tc.tile_pool(name="xin", bufs=B))
        outp = ctx.enter_context(tc.tile_pool(name="outp", bufs=3))
        work = ctx.enter_context(tc.tile_pool(name="work", bufs=3))
        small = ctx.enter_context(tc.tile_pool(name="small", bufs=4))
        ps_xt = ctx.enter_context(tc.psum_pool(name="ps_xt", bufs=2))
        ps_qk = ctx.enter_context(tc.psum_pool(name="ps_qk", bufs=4))
        ps_v = ctx.enter_context(tc.psum_pool(name="ps_v", bufs=2))
        if MANUAL:
            ctx.enter_context(tc.manual_schedule())

        tpos = const.tile([P, J], F32, name="tpos")
        nc.gpsimd.iota(tpos[:], pattern=[[1, J]], base=0, channel_multiplier=J, allow_small_or_imprecise_dtypes=True)
        ident = const.tile([P, P], F32, name="ident")
        make_identity(nc, ident[:])
        perm = const.tile([P, P], F32, name="perm")

        lam_bf = const.tile([P, 2], BF16, name="lam_bf")
        w_sb = const.tile([P, 6, C], BF16, name="w_sb")
        x_sb = [xin.tile([P, J, C], BF16, name="x_sb") for b in range(B)]
        ve_sb = [xin.tile([P, J, HD], BF16, name="ve_sb") for b in range(B)]
        for c0 in (0, C // 2):
            nc.sync.dma_start(out=w_sb[:, 0, c0 : c0 + C // 2], in_=w_v[:, 0, c0 : c0 + C // 2])
        for r in range(1, 4):
            nc.sync.dma_start(out=w_sb[:, r, :], in_=w_v[:, r, :])
        nc.sync.dma_start(out=x_sb[0][:, 0, :], in_=x_v[0][:, 0, :])
        nc.sync.dma_start(out=x_sb[0][:, 1, :], in_=x_v[0][:, 1, :])
        nc.sync.dma_start(out=w_sb[:, 4:6, :], in_=w_v[:, 4:6, :])
        nc.sync.dma_start(out=x_sb[0][:, 2:4, :], in_=x_v[0][:, 2:4, :])
        nc.sync.dma_start(out=x_sb[0][:, 4:6, :], in_=x_v[0][:, 4:6, :])
        nc.sync.dma_start(out=lam_bf[:], in_=lambdas.partition_broadcast(P))
        nc.sync.dma_start(out=ve_sb[0][:], in_=ve_v[0])
        nc.sync.dma_start(out=x_sb[0][:, 6:8, :], in_=x_v[0][:, 6:8, :])
        for b in range(1, B):
            nc.sync.dma_start(out=x_sb[b][:, 0:4, :], in_=x_v[b][:, 0:4, :])
            nc.sync.dma_start(out=ve_sb[b][:], in_=ve_v[b])
            nc.sync.dma_start(out=x_sb[b][:, 4:8, :], in_=x_v[b][:, 4:8, :])

        zero1 = const.tile([P, 1], F32, name="zero1")
        nc.vector.memset(zero1[:], 0.0)
        warm = const.tile([P, 1], F32, name="warm")
        nc.scalar.activation(out=warm[:], in_=zero1[:], func=ACT.Sin)
        ratio = (1.0 / 1024.0) ** (1.0 / 31.0)
        turns = const.tile([P, 32], F32, name="turns")
        for i in range(8):
            nc.vector.tensor_scalar_add(out=turns[:, i : i + 1], in0=zero1[:], scalar1=ratio ** i / (2.0 * math.pi))
        nc.vector.tensor_scalar_mul(out=turns[:, 8:16], in0=turns[:, 0:8], scalar1=ratio ** 8)
        nc.vector.tensor_copy(
            out=perm[:].rearrange("p (y z i) -> p y z i", y=2, z=2),
            in_=ident[:].rearrange("p (z y i) -> p y z i", y=2, z=2),
        )
        nc.vector.tensor_scalar_mul(out=turns[:, 16:32], in0=turns[:, 0:16], scalar1=ratio ** 16)
        ang = const.tile([P, J, 32], F32, name="ang")
        whole = const.tile([P, J, 32], I32, name="whole")
        negf = const.tile([P, J, 32], F32, name="negf")
        absf = const.tile([P, J, 32], F32, name="absf")
        halves = [slice(0, J // 2), slice(J // 2, J)]
        for js in halves:
            nc.vector.tensor_tensor(
                out=ang[:, js, :],
                in0=tpos[:, js].unsqueeze(2).to_broadcast([P, J // 2, 32]),
                in1=turns[:].unsqueeze(1).to_broadcast([P, J // 2, 32]),
                op=ALU.mult,
            )
        for js in halves:
            nc.vector.tensor_copy(out=whole[:, js, :], in_=ang[:, js, :])
        for js in halves:
            nc.vector.tensor_tensor(out=negf[:, js, :], in0=whole[:, js, :], in1=ang[:, js, :], op=ALU.subtract)
        for js in halves:
            nc.vector.scalar_tensor_tensor(
                out=absf[:, js, :].rearrange("p j i -> p (j i)"),
                in0=negf[:, js, :].rearrange("p j i -> p (j i)"),
                scalar=-1.0,
                in1=negf[:, js, :].rearrange("p j i -> p (j i)"),
                op0=ALU.mult,
                op1=ALU.max,
            )
        cs = const.tile([P, J, 2, 2, 32], F32, name="cs")
        nc.scalar.activation(out=cs[:, :, 1, 0, :], in_=negf[:], func=ACT.Sin, scale=2.0 * math.pi)
        nc.scalar.activation(
            out=cs[:, :, 0, 0, :], in_=absf[:], func=ACT.Sin, scale=-2.0 * math.pi, bias=0.5 * math.pi
        )
        nc.scalar.activation(out=warm[:], in_=zero1[:], func=ACT.Abs_reciprocal_sqrt, bias=1.0)
        nc.gpsimd.tensor_scalar(
            out=cs[:, :, 1, 1, :], in0=cs[:, :, 1, 0, :], scalar1=-1.0, scalar2=0.0, op0=ALU.mult, op1=ALU.add
        )
        nc.gpsimd.tensor_scalar(
            out=cs[:, :, 0, 1, :], in0=cs[:, :, 0, 0, :], scalar1=1.0, scalar2=0.0, op0=ALU.mult, op1=ALU.add
        )
        lam = const.tile([P, 2], F32, name="lam")

        wg = const.tile([P, 2, 3 * HD, 4], BF16, name="wg", align_bytes=64)
        wgf = wg[:].bitcast(F32)
        wc = const.tile([P, 2, 3 * HD], U32, name="wc", align_bytes=256)
        ws = const.tile([P, 2, 3 * HD], U8, name="ws", align_bytes=256)
        w_words = w_sb[:].bitcast(F32)

        def w_transpose(r):
            if r < 4:
                wt = ps_qk.tile([P, 4, P], F32, name="wt", tag="qk")
            else:
                wt = ps_v.tile([P, 4, P], F32, name="wt", tag="v")
            order = perm if r < 4 else ident
            for q in range(4):
                nc.tensor.transpose(wt[:, q, :], w_words[:, r, (q // 2) * 256 + q % 2 : (q // 2 + 1) * 256 : 2], order[:])
            return wt

        def w_copy(r, wt, eng):
            dst = wgf[:, :, r * P : (r + 1) * P, :]
            src = wt[:].rearrange("p (g u) n -> p g n u", u=2)
            if eng == "s":
                nc.scalar.copy(out=dst, in_=src)
            else:
                nc.vector.tensor_copy(out=dst, in_=src)

        def w_quant(g, n0, n1):
            nc.vector.quantize_mx(
                out=wc[:, g, n0:n1].bitcast(FP8X4),
                scales=ws[:, g, n0:n1],
                in_=wg[:, g, n0:n1, :].rearrange("p n t -> p (n t)"),
            )

        xt_t = {}
        grp_t = {}
        xc_t = {}
        xs_t = {}
        qk_t = {}
        v_t = {}
        ss_t = {}
        junk_t = {}
        t_t = {}
        r_t = {}
        qk_sb = {}
        v_sb = {}

        def where(n):
            return n // 4, 2 * (n % 4)

        def transposes(n, s):
            b, j0 = where(n)
            xw = x_sb[b][:].bitcast(F32)
            xt = ps_xt.tile([P, 4, P], F32, name="xt", tag="xt")
            for q in range(4):
                nc.tensor.transpose(xt[:, q, :], xw[:, j0 + s, (q // 2) * 256 + q % 2 : (q // 2 + 1) * 256 : 2], ident[:])
            xt_t[(n, s)] = xt

        def x_copy(n, s, eng):
            if s == 0:
                grp_t[n] = work.tile([P, 2, 2, P, 4], BF16, name="grp", align_bytes=64)
            dst = grp_t[n][:].bitcast(F32)[:, s, :, :, :]
            src = xt_t[(n, s)][:].rearrange("p (g u) m -> p g m u", u=2)
            if eng == "s":
                nc.scalar.copy(out=dst, in_=src)
            else:
                nc.vector.tensor_copy(out=dst, in_=src)

        def x_quant(n, s0=0, s1=2):
            if s0 == 0:
                xc_t[n] = work.tile([P, 2, 2, P], U32, name="xc", align_bytes=256)
                xs_t[n] = work.tile([P, 2, 2, P], U8, name="xs", align_bytes=256)
            nc.vector.quantize_mx(
                out=xc_t[n][:, s0:s1, :, :].rearrange("p s g m -> p (s g m)").bitcast(FP8X4),
                scales=xs_t[n][:, s0:s1, :, :].rearrange("p s g m -> p (s g m)"),
                in_=grp_t[n][:, s0:s1, :, :, :].rearrange("p s g m t -> p (s g m t)"),
            )

        def matmul_qk(n, s):
            xc = xc_t[n]
            xs = xs_t[n]
            qkps = ps_qk.tile([P, 2 * HD], F32, name="qkps", tag="qk")
            qk_t[(n, s)] = qkps
            for g in range(2):
                nc.tensor.matmul_mx(
                    out=qkps[:],
                    lhsT=xc[:, s, g, :].bitcast(FP8X4),
                    lhsT_scale=xs[:, s, g, :],
                    rhs=wc[:, g, 0 : 2 * HD].bitcast(FP8X4),
                    rhs_scale=ws[:, g, 0 : 2 * HD],
                    start=(g == 0),
                    stop=(g == 1),
                )

        def matmul_v(n):
            xc = xc_t[n]
            xs = xs_t[n]
            vps = ps_v.tile([P, 2, HD], F32, name="vps", tag="v")
            v_t[n] = vps
            for s in range(2):
                for g in range(2):
                    nc.tensor.matmul_mx(
                        out=vps[:, s, :],
                        lhsT=xc[:, s, g, :].bitcast(FP8X4),
                        lhsT_scale=xs[:, s, g, :],
                        rhs=wc[:, g, 2 * HD : 3 * HD].bitcast(FP8X4),
                        rhs_scale=ws[:, g, 2 * HD : 3 * HD],
                        start=(g == 0),
                        stop=(g == 1),
                    )

        def ve_scale(n):
            b, j0 = where(n)
            if j0 == 0:
                v_sb[b] = outp.tile([P, J, HD], F32, name="v_sb")
            for s in range(2):
                nc.gpsimd.tensor_scalar(
                    out=v_sb[b][:, j0 + s, :],
                    in0=ve_sb[b][:, j0 + s, :],
                    scalar1=lam[:, 1:2],
                    scalar2=0.0,
                    op0=ALU.mult,
                    op1=ALU.add,
                )

        def v_blend(n):
            b, j0 = where(n)
            dst = v_sb[b][:, j0 : j0 + 2, :].rearrange("p j f -> p (j f)")
            nc.vector.scalar_tensor_tensor(
                out=dst,
                in0=v_t[n][:].rearrange("p s f -> p (s f)"),
                scalar=lam[:, 0:1],
                in1=dst,
                op0=ALU.mult,
                op1=ALU.add,
            )

        def sumsq(n, s):
            if s == 0:
                ss_t[n] = small.tile([P, 8], F32, name="ss")
                r_t[n] = small.tile([P, 8], F32, name="r")
                junk_t[n] = work.tile([P, 8, D], BF16, name="junk")
            for q in range(4):
                i = 4 * s + q
                nc.scalar.activation(
                    out=junk_t[n][:, i, :],
                    in_=qk_t[(n, s)][:, q * D : (q + 1) * D],
                    func=ACT.Square,
                    accum_out=ss_t[n][:, i : i + 1],
                )

        def rstd(n, s):
            nc.scalar.activation(
                out=r_t[n][:, 4 * s : 4 * s + 4],
                in_=ss_t[n][:, 4 * s : 4 * s + 4],
                func=ACT.Abs_reciprocal_sqrt,
                scale=1.0 / D,
                bias=EPS,
            )

        def products(n, s):
            b, j0 = where(n)
            if s == 0:
                t_t[n] = work.tile([P, 2, 2, 2, H, D // 2], F32, name="t")
            for q in range(4):
                nc.vector.scalar_tensor_tensor(
                    out=t_t[n][:, :, q // 2, s, q % 2, :],
                    in0=qk_t[(n, s)][:, q * D : q * D + D // 2].unsqueeze(1).to_broadcast([P, 2, D // 2]),
                    scalar=r_t[n][:, 4 * s + q : 4 * s + q + 1],
                    in1=cs[:, j0 + s, :, :, :].rearrange("p e z i -> p e (z i)"),
                    op0=ALU.mult,
                    op1=ALU.mult,
                )

        def unrotated(n, s):
            b, j0 = where(n)
            out = qk_sb[b][:, :, j0 + s, :].rearrange("p a (h z f) -> p a h z f", h=H, z=2)[:, :, :, :, 32:64]
            u = qk_t[(n, s)][:].rearrange("p (a h y z i) -> p a h y z i", a=2, h=H, y=2, z=2)[:, :, :, 1, :, :]
            for a in range(2):
                for h in range(H):
                    q = 4 * s + 2 * a + h
                    nc.scalar.activation(
                        out=out[:, a, h, :, :], in_=u[:, a, h, :, :], func=ACT.Copy, scale=r_t[n][:, q : q + 1]
                    )

        def combine(n, engines):
            b, j0 = where(n)
            y = qk_sb[b][:, :, j0 : j0 + 2, :].rearrange("p a j (h z f) -> p a (j h) z f", h=H, z=2)
            t = t_t[n][:].rearrange("p e a s h (z i) -> p e a (s h) z i", z=2)
            for z in range(2):
                engines[z].tensor_tensor(
                    out=y[:, :, :, z, 0:32], in0=t[:, 0, :, :, z, :], in1=t[:, 1, :, :, 1 - z, :], op=ALU.add
                )

        def combine_tile(n, s, eng):
            b, j0 = where(n)
            y = qk_sb[b][:, :, j0 + s, :].rearrange("p a (h z f) -> p a h z f", h=H, z=2)
            t = t_t[n][:, :, :, s, :, :].rearrange("p e a h (z i) -> p e a h z i", z=2)
            for z in range(2):
                eng.tensor_tensor(
                    out=y[:, :, :, z, 0:32], in0=t[:, 0, :, :, z, :], in1=t[:, 1, :, :, 1 - z, :], op=ALU.add
                )

        def store_qk(b, js):
            nc.sync.dma_start(out=o_v[0][b][:, js, :], in_=qk_sb[b][:, 0, js, :])
            nc.sync.dma_start(out=o_v[1][b][:, js, :], in_=qk_sb[b][:, 1, js, :])

        def store_v(b, js):
            nc.sync.dma_start(out=o_v[2][b][:, js, :], in_=v_sb[b][:, js, :])

        wts = [w_transpose(r) for r in range(4)]
        transposes(0, 0)
        transposes(0, 1)
        wts.append(w_transpose(4))
        wts.append(w_transpose(5))
        w_copy(0, wts[0], "v")
        w_copy(1, wts[1], "s")
        w_copy(2, wts[2], "v")
        w_copy(3, wts[3], "s")
        w_quant(0, 0, HD)
        w_quant(1, 0, HD)
        x_copy(0, 0, "s")
        w_quant(0, HD, 2 * HD)
        w_quant(1, HD, 2 * HD)
        x_quant(0, 0, 1)
        x_copy(0, 1, "s")
        w_copy(4, wts[4], "v")
        x_quant(0, 1, 2)
        w_copy(5, wts[5], "s")
        transposes(1, 0)
        transposes(1, 1)
        w_quant(0, 2 * HD, 3 * HD)
        w_quant(1, 2 * HD, 3 * HD)
        x_copy(1, 0, "s")
        x_copy(1, 1, "v")
        nc.vector.tensor_copy(out=lam[:], in_=lam_bf[:])
        x_quant(1)
        for n in range(3):
            ve_scale(n)

        for n in range(NPAIR):
            b, j0 = where(n)
            if j0 == 0:
                qk_sb[b] = outp.tile([P, 2, J, HD], F32, name="qk_sb")
            matmul_qk(n, 0)
            matmul_qk(n, 1)
            if n + 2 < NPAIR:
                transposes(n + 2, 0)
                transposes(n + 2, 1)
            matmul_v(n)
            sumsq(n, 0)
            sumsq(n, 1)
            rstd(n, 0)
            if n + 2 < NPAIR:
                x_copy(n + 2, 0, "s")
            rstd(n, 1)
            if n == NPAIR - 1:
                break
            if n + 2 < NPAIR:
                x_copy(n + 2, 1, "v")
            unrotated(n, 0)
            unrotated(n, 1)
            products(n, 0)
            products(n, 1)
            if n + 2 < NPAIR:
                x_quant(n + 2)
            v_blend(n)
            combine(n, (nc.gpsimd, nc.vector if n == NPAIR - 2 else nc.gpsimd))
            if n + 3 < NPAIR:
                ve_scale(n + 3)
            if n < NPAIR - 4:
                if j0 % 4 == 2:
                    store_v(b, slice(j0 - 2, j0 + 2))
                    store_qk(b, slice(j0 - 2, j0 + 2))
            else:
                store_v(b, slice(j0, j0 + 2))
                store_qk(b, slice(j0, j0 + 2))

        last = NPAIR - 1
        b, j0 = where(last)
        own = slice(j0, j0 + 2)
        v_blend(last)
        store_v(b, own)
        products(last, 0)
        unrotated(last, 0)
        products(last, 1)
        unrotated(last, 1)
        combine_tile(last, 0, nc.vector)
        store_qk(b, slice(j0, j0 + 1))
        combine_tile(last, 1, nc.vector)
        store_qk(b, slice(j0 + 1, j0 + 2))
